import numpy as np
import ml_dtypes


def mxq(x, axis, fmt="e4m3"):
    dtype, down = {"e4m3": (ml_dtypes.float8_e4m3fn, 7), "e5m2": (ml_dtypes.float8_e5m2, 14)}[fmt]
    v = np.moveaxis(np.asarray(x, np.float32).astype(ml_dtypes.bfloat16).astype(np.float64), axis, -1)
    blocks = v.reshape(v.shape[:-1] + (-1, 32))
    amax = np.abs(blocks).max(-1, keepdims=True)
    byte = np.maximum(np.where(amax > 0, np.frexp(amax)[1] - 1 + 127, 0) - down, 1)
    scale = np.exp2(byte - 127.0)
    codes = (blocks / scale).astype(np.float32).astype(dtype).astype(np.float64)
    return np.moveaxis((codes * scale).reshape(v.shape), -1, axis)


WIDE = False


def mx_kscale(k):
    if not WIDE:
        return np.ones(k)
    levels = np.array([10, -10, 5, -5, 0])
    if k % 512:
        return np.exp2(np.random.permutation(np.resize(levels, k // 32))).repeat(32)
    a = np.empty((k // 512, 16))
    for p in range(k // 512):
        a[p, :8] = np.random.permutation(np.resize(levels, 8))
        for g in range(8):
            far = levels[np.abs(levels - a[p, g]) >= 10]
            a[p, g + 8] = far[np.random.randint(len(far))]
    return np.exp2(a.ravel()).repeat(32)


BF16 = ml_dtypes.bfloat16


def bf(x):
    return np.asarray(x, np.float32).astype(BF16)


def f64(x):
    return np.asarray(x).astype(np.float64)


B, S, H, NH, DH, G = 1, 512, 2048, 16, 128, 4
NKV = NH // G
ROPE_THETA = 10000.0


def rope(x):
    inv_freq = 1.0 / ROPE_THETA ** (np.arange(0, DH, 2) / DH)
    angles = np.arange(S)[:, None] * inv_freq[None, :]
    cos = np.cos(angles)[None, :, None, :]
    sin = np.sin(angles)[None, :, None, :]
    x1, x2 = np.split(x, 2, axis=-1)
    return np.concatenate([x1 * cos - x2 * sin, x1 * sin + x2 * cos], axis=-1)


def draw0():
    s = mx_kscale(H)
    return {
        "hidden_states": bf(np.random.standard_normal((B, S, H)) * s),
        "Wq": bf(np.random.standard_normal((H, NH * DH)) * 1.4 / np.sqrt(H) / s[:, None]),
        "bq": bf(np.random.standard_normal(NH * DH) * 0.2),
        "Wk": bf(np.random.standard_normal((H, NKV * DH)) * 1.4 / np.sqrt(H) / s[:, None]),
        "bk": bf(np.random.standard_normal(NKV * DH) * 0.2),
        "Wv": bf(np.random.standard_normal((H, NKV * DH)) / np.sqrt(H) / s[:, None]),
        "bv": bf(np.random.standard_normal(NKV * DH) * 0.2),
    }


def core(hidden_states, Wq, bq, Wk, bk, Wv, bv):
    xq = mxq(f64(hidden_states), 2, "e4m3")
    q = ((xq @ mxq(f64(Wq), 0, "e4m3")) + f64(bq)).reshape(B, S, NH, DH)
    k = ((xq @ mxq(f64(Wk), 0, "e4m3")) + f64(bk)).reshape(B, S, NKV, DH)
    v = ((xq @ mxq(f64(Wv), 0, "e4m3")) + f64(bv)).reshape(B, S, NKV, DH)
    q = rope(q)
    k = rope(k)
    return q.transpose(0, 2, 1, 3), k.transpose(0, 2, 1, 3), v.transpose(0, 2, 1, 3)


def e4m3fn_bytes(y):
    return np.clip(np.asarray(y, np.float64), -448.0, 448.0).astype(np.float32).astype(ml_dtypes.float8_e4m3fn).view(np.uint8)


def e4m3fn_values(b):
    return np.asarray(b, np.uint8).view(ml_dtypes.float8_e4m3fn).astype(np.float64)


def setup_inputs():
    d = draw0()
    x0 = np.asarray(d['Wq']).astype(np.float64)
    s = (np.max(np.abs(x0), axis=(1,), keepdims=True) / 448.0).astype(np.float32)
    out = {}
    for k, v in d.items():
        if k == 'Wq':
            out['Wq_bytes'] = e4m3fn_bytes(x0 / s.astype(np.float64))
            out['Wq_scale'] = s
        else:
            out[k] = v
    return out


def reference(hidden_states, Wq_bytes, Wq_scale, bq, Wk, bk, Wv, bv):
    return core(hidden_states, e4m3fn_values(Wq_bytes) * Wq_scale.astype(np.float64), bq, Wk, bk, Wv, bv)

@@ -1,0 +1,436 @@
+from contextlib import ExitStack
+import math
+
+import concourse.mybir as mybir
+from concourse.masks import make_identity
+
+FLOPS = 2 * 512 * 2048 * 3072
+
+F32 = mybir.dt.float32
+BF16 = mybir.dt.bfloat16
+I32 = mybir.dt.int32
+U32 = mybir.dt.uint32
+U8 = mybir.dt.uint8
+FP8 = mybir.dt.float8_e4m3fn
+FP8X4 = mybir.dt.float8_e4m3fn_x4
+ALU = mybir.AluOpType
+ACT = mybir.ActivationFunctionType
+
+P = 128
+PACK = 4
+PASSES = 4
+TOK = 512
+HID = 2048
+DH = 128
+CH = 512
+ROPE_THETA = 10000.0
+TWO_PI_HI = 6.28125
+TWO_PI_LO = 2.0 * math.pi - TWO_PI_HI
+
+NV_EARLY = 92
+NV_VALUE = 128
+NV_LATE = 44
+NG = 24
+PLANES_PER_SLOT = 3
+MANUAL = True
+
+
+def tile_autoreggqaattention_pa_kernel(
+    tc, hidden_states, Wq_bytes, Wq_scale, bq, Wk, bk, Wv, bv, out_0, out_1, out_2
+):
+    nc = tc.nc
+    with ExitStack() as ctx:
+        const = ctx.enter_context(tc.tile_pool(name="const", bufs=1))
+        tmp = ctx.enter_context(tc.tile_pool(name="tmp", bufs=1))
+        xin = ctx.enter_context(tc.tile_pool(name="xin", bufs=1))
+        wbp = ctx.enter_context(tc.tile_pool(name="wbp", bufs=1))
+        rawp = ctx.enter_context(tc.tile_pool(name="rawp", bufs=1))
+        widep = ctx.enter_context(tc.tile_pool(name="widep", bufs=3))
+        ilp = ctx.enter_context(tc.tile_pool(name="ilp", bufs=2))
+        cod = ctx.enter_context(tc.tile_pool(name="cod", bufs=4))
+        xgp = ctx.enter_context(tc.tile_pool(name="xgp", bufs=4))
+        keep = ctx.enter_context(tc.tile_pool(name="keep", bufs=1))
+        ep = ctx.enter_context(tc.tile_pool(name="ep", bufs=3))
+        outp = ctx.enter_context(tc.tile_pool(name="outp", bufs=4))
+        ps_acc = ctx.enter_context(tc.psum_pool(name="ps_acc", bufs=4))
+        ps_tr = ctx.enter_context(tc.psum_pool(name="ps_tr", bufs=4))
+
+        wscale = const.tile([P, PASSES, PACK], F32, name="wscale")
+        nc.sync.dma_start(
+            out=wscale[:],
+            in_=Wq_scale.rearrange("(g p t) o -> p g (t o)", g=PASSES, p=P, t=PACK),
+        )
+        wq_view = Wq_bytes.rearrange("(g p t) n -> g p t n", g=PASSES, p=P, t=PACK)
+        wk_view = Wk.rearrange("(g p t) n -> g p t n", g=PASSES, p=P, t=PACK)
+        wv_view = Wv.rearrange("(g p t) n -> g p t n", g=PASSES, p=P, t=PACK)
+        hs = hidden_states[0].rearrange("(p a) h -> a p h", a=4)
+
+        wb = []
+        for c in range(4):
+            wb_c = wbp.tile([P, PASSES * PACK, CH], U8, name="wb%d" % c, tag="wb%d" % c)
+            wb.append(wb_c)
+        raw_k = rawp.tile([P, PASSES * PACK, CH], BF16, name="raw_k", tag="raw_k")
+        raw_v = rawp.tile([P, PASSES * PACK, CH], BF16, name="raw_v", tag="raw_v")
+        x_sb = []
+        for a in range(4):
+            x_a = xin.tile([P, HID], BF16, name="x%d" % a, tag="x%d" % a)
+            x_sb.append(x_a)
+
+        def load_q(c):
+            for g in range(PASSES):
+                nc.sync.dma_start(
+                    out=wb[c][:, PACK * g : PACK * (g + 1), :],
+                    in_=wq_view[g][:, :, c * CH : (c + 1) * CH],
+                )
+
+        def load_kv(dst, view):
+            for g in range(PASSES):
+                nc.sync.dma_start(out=dst[:, PACK * g : PACK * (g + 1), :], in_=view[g])
+
+        brow = const.tile([P, P], BF16, name="brow")
+        nc.vector.memset(brow[:], 0.0)
+        load_q(0)
+        nc.sync.dma_start(out=brow[0:16, :], in_=bq.rearrange("(h f) -> h f", f=DH))
+        nc.sync.dma_start(out=brow[16:20, :], in_=bk.rearrange("(h f) -> h f", f=DH))
+        nc.sync.dma_start(out=brow[20:24, :], in_=bv.rearrange("(h f) -> h f", f=DH))
+        for a in range(4):
+            nc.sync.dma_start(out=x_sb[a][:], in_=hs[a])
+        load_q(1)
+        load_kv(raw_k, wk_view)
+        load_q(2)
+        load_kv(raw_v, wv_view)
+        load_q(3)
+
+        zero1 = const.tile([P, 1], F32, name="zero1")
+        nc.vector.memset(zero1[:], 0.0)
+        warm = const.tile([P, 1], F32, name="warm")
+        nc.scalar.activation(out=warm[:], in_=zero1[:], func=ACT.Sin)
+
+        ident = const.tile([P, P], F32, name="ident")
+        make_identity(nc, ident[:])
+        ident_bf = const.tile([P, P], BF16, name="ident_bf")
+        make_identity(nc, ident_bf[:])
+        swap = const.tile([P, P], F32, name="swap")
+        nc.gpsimd.tensor_copy(out=swap[:, 0:64], in_=ident[:, 64:128])
+        nc.gpsimd.tensor_copy(out=swap[:, 64:128], in_=ident[:, 0:64])
+
+        pidx = tmp.tile([P, 7], I32, name="pidx")
+        nc.gpsimd.iota(pidx[:], pattern=[[0, 7]], base=0, channel_multiplier=1)
+        shft = tmp.tile([P, 7], I32, name="shft")
+        nc.gpsimd.iota(shft[:], pattern=[[1, 7]], base=0, channel_multiplier=0)
+        tok = tmp.tile([P, TOK], F32, name="tok")
+        nc.gpsimd.iota(
+            tok[:],
+            pattern=[[1, 4], [4, P]],
+            base=0,
+            channel_multiplier=0,
+            allow_small_or_imprecise_dtypes=True,
+        )
+        bsh = tmp.tile([P, 7], I32, name="bsh")
+        nc.vector.tensor_tensor(out=bsh[:], in0=pidx[:], in1=shft[:], op=ALU.logical_shift_right)
+        bit_i = tmp.tile([P, 7], I32, name="bit_i")
+        nc.vector.tensor_scalar(out=bit_i[:], in0=bsh[:], scalar1=1, scalar2=None, op0=ALU.bitwise_and)
+        bit = tmp.tile([P, 7], F32, name="bit")
+        nc.vector.tensor_copy(out=bit[:], in_=bit_i[:])
+        nbit = tmp.tile([P, 7], F32, name="nbit")
+        nc.vector.tensor_scalar(
+            out=nbit[:], in0=bit[:], scalar1=-1.0, scalar2=1.0, op0=ALU.mult, op1=ALU.add
+        )
+        fac = tmp.tile([P, 6], F32, name="fac")
+        for b in range(6):
+            nc.vector.scalar_tensor_tensor(
+                out=fac[:, b : b + 1],
+                in0=bit[:, b : b + 1],
+                scalar=ROPE_THETA ** (-(2.0**b) / 64.0),
+                in1=nbit[:, b : b + 1],
+                op0=ALU.mult,
+                op1=ALU.add,
+            )
+        f3 = tmp.tile([P, 3], F32, name="f3")
+        nc.vector.tensor_tensor(out=f3[:], in0=fac[:, 0:3], in1=fac[:, 3:6], op=ALU.mult)
+        f1 = tmp.tile([P, 1], F32, name="f1")
+        nc.vector.tensor_tensor(out=f1[:], in0=f3[:, 0:1], in1=f3[:, 1:2], op=ALU.mult)
+        freq = tmp.tile([P, 1], F32, name="freq")
+        nc.vector.tensor_tensor(out=freq[:], in0=f1[:], in1=f3[:, 2:3], op=ALU.mult)
+        turns = tmp.tile([P, 1], F32, name="turns")
+        nc.vector.tensor_scalar(
+            out=turns[:], in0=freq[:], scalar1=1.0 / (2.0 * math.pi), scalar2=None, op0=ALU.mult
+        )
+        sgn2 = tmp.tile([P, 1], F32, name="sgn2")
+        nc.vector.tensor_scalar(
+            out=sgn2[:], in0=bit[:, 6:7], scalar1=-4.0, scalar2=2.0, op0=ALU.mult, op1=ALU.add
+        )
+
+        n_i = tmp.tile([P, TOK], I32, name="n_i")
+        nc.vector.tensor_scalar(out=n_i[:], in0=tok[:], scalar1=turns[:], scalar2=None, op0=ALU.mult)
+        ang = tmp.tile([P, TOK], F32, name="ang")
+        nc.scalar.activation(out=ang[:], in_=tok[:], func=ACT.Copy, scale=freq[:])
+        r1 = tmp.tile([P, TOK], F32, name="r1")
+        nc.vector.scalar_tensor_tensor(
+            out=r1[:], in0=n_i[:], scalar=-TWO_PI_HI, in1=ang[:], op0=ALU.mult, op1=ALU.add
+        )
+        red = tmp.tile([P, TOK], F32, name="red")
+        nc.vector.scalar_tensor_tensor(
+            out=red[:], in0=n_i[:], scalar=-TWO_PI_LO, in1=r1[:], op0=ALU.mult, op1=ALU.add
+        )
+        wide = {}
+
+        def widen(c, g, t, lo, hi, on_vector):
+            if c not in wide:
+                wide_c = widep.tile([P, PASSES * PACK, CH], BF16, name="wide", tag="wide")
+                wide[c] = wide_c
+            k = PACK * g + t
+            if on_vector:
+                nc.vector.tensor_scalar(
+                    out=wide[c][:, k, lo:hi],
+                    in0=wb[c][:, k, lo:hi].bitcast(FP8),
+                    scalar1=wscale[:, g, t : t + 1],
+                    scalar2=None,
+                    op0=ALU.mult,
+                )
+            else:
+                nc.scalar.activation(
+                    out=wide[c][:, k, lo:hi],
+                    in_=wb[c][:, k, lo:hi].bitcast(FP8),
+                    func=ACT.Copy,
+                    scale=wscale[:, g, t : t + 1],
+                )
+
+        def widen_head(hh, on_vector):
+            for g in range(PASSES):
+                for t in range(PACK):
+                    widen(0, g, t, hh * DH, (hh + 1) * DH, on_vector)
+
+        pending = [(c, g, t) for c in (1, 2, 3) for g in range(PASSES) for t in range(PACK)]
+        widen_head(0, True)
+        widen_head(1, False)
+
+        ared = tmp.tile([P, TOK], F32, name="ared")
+        nc.scalar.activation(out=ared[:], in_=red[:], func=ACT.Abs)
+        s_h = tmp.tile([P, TOK], F32, name="s_h")
+        nc.scalar.activation(out=s_h[:], in_=red[:], func=ACT.Sin, scale=0.5)
+        c_h = tmp.tile([P, TOK], F32, name="c_h")
+        nc.scalar.activation(out=c_h[:], in_=ared[:], func=ACT.Sin, scale=-0.5, bias=math.pi / 2.0)
+        stab = const.tile([P, TOK], F32, name="stab")
+        nc.vector.scalar_tensor_tensor(
+            out=stab[:], in0=s_h[:], scalar=sgn2[:], in1=c_h[:], op0=ALU.mult, op1=ALU.mult
+        )
+        sq = tmp.tile([P, TOK], F32, name="sq")
+        nc.vector.tensor_tensor(out=sq[:], in0=s_h[:], in1=s_h[:], op=ALU.mult)
+        ctab = const.tile([P, TOK], F32, name="ctab")
+        nc.vector.tensor_scalar(
+            out=ctab[:], in0=sq[:], scalar1=-2.0, scalar2=1.0, op0=ALU.mult, op1=ALU.add
+        )
+
+        widen_head(2, False)
+        widen_head(3, False)
+
+        bias_ps = ps_tr.tile([P, P], BF16, name="bias_ps", tag="tr")
+        nc.tensor.transpose(bias_ps[:], brow[:], ident_bf[:])
+        bias = const.tile([P, 24], F32, name="bias")
+        nc.vector.tensor_copy(out=bias[:], in_=bias_ps[:, 0:24])
+
+        xc = keep.tile([P, PASSES, TOK], U32, name="xc", align_bytes=64)
+        xs = keep.tile([P, PASSES, TOK], U8, name="xs", align_bytes=64)
+        for jp in range(2):
+            banks = []
+            for g in range(PASSES):
+                xt = ps_tr.tile([P, 2, 256], F32, name="xt", tag="tr")
+                banks.append(xt)
+            for al in range(2):
+                words = x_sb[2 * jp + al][:].bitcast(F32)
+                for g in range(PASSES):
+                    for u in range(2):
+                        nc.tensor.transpose(
+                            banks[g][:, u, al * P : (al + 1) * P],
+                            words[:, 256 * g + u : 256 * (g + 1) : 2],
+                            ident[:],
+                        )
+            grouped = []
+            for step in range(PASSES + 1):
+                if step < PASSES:
+                    g = step
+                    xg = xgp.tile([P, 256, PACK], BF16, name="xg", tag="xg", align_bytes=64)
+                    grouped.append(xg)
+                    xg_words = xg[:].rearrange("p r t -> p (r t)").bitcast(F32).rearrange("p (r u) -> p r u", u=2)
+                    if jp == 1 and g % 2 == 1:
+                        nc.scalar.copy(out=xg_words, in_=banks[g][:].rearrange("p u r -> p r u"))
+                    else:
+                        nc.vector.tensor_copy(out=xg_words, in_=banks[g][:].rearrange("p u r -> p r u"))
+                if step > 0:
+                    g = step - 1
+                    cols = slice(jp * 256, (jp + 1) * 256)
+                    nc.vector.quantize_mx(
+                        out=xc[:, g, cols].bitcast(FP8X4),
+                        scales=xs[:, g, cols],
+                        in_=grouped[g][:].rearrange("p r t -> p (r t)"),
+                    )
+
+        oq = out_0[0].rearrange("h (p a) f -> h p (a f)", a=4)
+        ok = out_1[0].rearrange("h (p a) f -> h p (a f)", a=4)
+        ov = out_2[0].rearrange("h (p a) f -> h p (a f)", a=4)
+        heads = []
+        for kind, c in (("q", 0), ("k", 0), ("q", 1), ("v", 0), ("q", 2), ("q", 3)):
+            for hh in range(4):
+                heads.append((kind, c, hh))
+
+        n_heads = len(heads)
+        state = {}
+
+        def source(j):
+            kind, c, hh = heads[j]
+            if kind == "q":
+                return wide[c], 4 * c + hh, oq[4 * c + hh]
+            if kind == "k":
+                return raw_k, 16 + hh, ok[hh]
+            return raw_v, 20 + hh, ov[hh]
+
+        def n_gpsimd(j):
+            if j >= 3 and heads[j - 3][0] != "v":
+                return NG
+            return 0
+
+        def n_vector(j):
+            if heads[j][0] == "v":
+                return NV_VALUE - n_gpsimd(j)
+            if j < 16:
+                return NV_EARLY - (2 * n_gpsimd(j)) // 3
+            return NV_LATE - n_gpsimd(j) // 2
+
+        def il_tile(j):
+            if ("il", j) not in state:
+                il = ilp.tile([P, PASSES, DH, PACK], BF16, name="il", tag="il", align_bytes=64)
+                state[("il", j)] = il
+            return state[("il", j)]
+
+        def il_view(j, lo, hi):
+            src = source(j)[0]
+            hh = heads[j][2]
+            return src[:, :, hh * DH + lo : hh * DH + hi].rearrange("p (g t) (c i) -> p g c t i", t=PACK, i=4)
+
+        def il_gpsimd(j):
+            lo = n_vector(j)
+            hi = lo + n_gpsimd(j)
+            if hi > lo:
+                src = source(j)[0]
+                hh = heads[j][2]
+                nc.gpsimd.tensor_scalar(
+                    out=il_tile(j)[:, :, lo:hi, :],
+                    in0=src[:, :, hh * DH + lo : hh * DH + hi].rearrange("p (g t) n -> p g n t", t=PACK),
+                    scalar1=1.0,
+                    scalar2=0.0,
+                    op0=ALU.mult,
+                    op1=ALU.add,
+                )
+
+        def il_scalar(j):
+            nv = n_vector(j) + n_gpsimd(j)
+            if nv < DH:
+                nc.scalar.copy(
+                    out=il_tile(j)[:, :, nv:DH, :].rearrange("p g (c i) t -> p g c t i", i=4), in_=il_view(j, nv, DH)
+                )
+
+        def il_vector(j):
+            nv = n_vector(j)
+            nc.vector.tensor_copy(
+                out=il_tile(j)[:, :, 0:nv, :].rearrange("p g (c i) t -> p g c t i", i=4), in_=il_view(j, 0, nv)
+            )
+
+        def quant(j):
+            wc = cod.tile([P, PASSES * DH], U32, name="wc", tag="wc", align_bytes=64)
+            ws = cod.tile([P, PASSES * DH], U8, name="ws", tag="ws", align_bytes=64)
+            nc.vector.quantize_mx(
+                out=wc[:].bitcast(FP8X4),
+                scales=ws[:],
+                in_=il_tile(j)[:].rearrange("p g n t -> p (g n t)"),
+            )
+            state[("wc", j)] = wc
+            state[("ws", j)] = ws
+
+        def mx(j):
+            acc = ps_acc.tile([P, TOK], F32, name="acc", tag="acc")
+            wc, ws = state[("wc", j)], state[("ws", j)]
+            for g in range(PASSES):
+                cols = slice(g * DH, (g + 1) * DH)
+                nc.tensor.matmul_mx(
+                    out=acc[:],
+                    lhsT=wc[:, cols].bitcast(FP8X4),
+                    lhsT_scale=ws[:, cols],
+                    rhs=xc[:, g, :].bitcast(FP8X4),
+                    rhs_scale=xs[:, g, :],
+                    start=(g == 0),
+                    stop=(g == PASSES - 1),
+                )
+            state[("acc", j)] = acc
+
+        def rope(j):
+            acc = state[("acc", j)]
+            bcol = source(j)[1]
+            b_ap = bias[:, bcol : bcol + 1]
+            u_t = ep.tile([P, TOK], F32, name="u_t", tag="u_t")
+            state[("u", j)] = u_t
+            if heads[j][0] == "v":
+                nc.vector.tensor_scalar(out=u_t[:], in0=acc[:], scalar1=b_ap, scalar2=None, op0=ALU.add)
+                return
+            w_t = ep.tile([P, TOK], F32, name="w_t", tag="w_t")
+            state[("w", j)] = w_t
+            nc.vector.scalar_tensor_tensor(
+                out=u_t[:], in0=acc[:], scalar=b_ap, in1=ctab[:], op0=ALU.add, op1=ALU.mult
+            )
+            nc.vector.scalar_tensor_tensor(
+                out=w_t[:], in0=acc[:], scalar=b_ap, in1=stab[:], op0=ALU.add, op1=ALU.mult
+            )
+
+        def tback(j):
+            tr = ps_tr.tile([P, TOK], F32, name="tr", tag="tr")
+            state[("tr", j)] = tr
+            u_t = state[("u", j)]
+            for a in range(4):
+                blk = slice(a * P, (a + 1) * P)
+                if heads[j][0] == "v":
+                    nc.tensor.transpose(tr[:, blk], u_t[:, blk], ident[:])
+                else:
+                    w_t = state[("w", j)]
+                    nc.tensor.matmul(
+                        tr[:, blk], lhsT=u_t[:, blk], rhs=ident[:], start=True, stop=False, is_transpose=True
+                    )
+                    nc.tensor.matmul(
+                        tr[:, blk], lhsT=w_t[:, blk], rhs=swap[:], start=False, stop=True, is_transpose=True
+                    )
+
+        def evac(j):
+            ob = outp.tile([P, TOK], F32, name="ob", tag="ob")
+            nc.scalar.copy(out=ob[:], in_=state[("tr", j)][:])
+            nc.sync.dma_start(out=source(j)[2], in_=ob[:])
+
+        def live(j):
+            return 0 <= j < n_heads
+
+        if MANUAL:
+            ctx.enter_context(tc.manual_schedule())
+        next_plane = 0
+        il_scalar(0)
+        for i in range(-2, n_heads + 2):
+            if live(i - 1) and i < n_heads - 3:
+                tback(i - 1)
+            if live(i + 1):
+                mx(i + 1)
+            if live(i - 1) and i >= n_heads - 3:
+                tback(i - 1)
+            if live(i + 3):
+                il_gpsimd(i + 3)
+            if live(i + 2):
+                il_vector(i + 2)
+            if live(i):
+                rope(i)
+            if live(i + 2):
+                quant(i + 2)
+            for j in range(PLANES_PER_SLOT):
+                if next_plane < len(pending):
+                    pc, pg, pt = pending[next_plane]
+                    next_plane += 1
+                    widen(pc, pg, pt, 0, CH, False)
+            if live(i + 3):
+                il_scalar(i + 3)
+            if live(i - 1):
+                evac(i - 1)

@@ -19,6 +19,7 @@ ACT = mybir.ActivationFunctionType
 P = 128
 PACK = 4
 PASSES = 4
+PLANES = PASSES * PACK
 TOK = 512
 HID = 2048
 DH = 128
@@ -27,12 +28,16 @@ ROPE_THETA = 10000.0
 TWO_PI_HI = 6.28125
 TWO_PI_LO = 2.0 * math.pi - TWO_PI_HI
 
-NV_EARLY = 92
-NV_VALUE = 128
-NV_LATE = 44
-NG = 24
-PLANES_PER_SLOT = 3
-MANUAL = True
+UNIT_SIZES = (2, 2, 2, 2, 2, 2, 2, 2, 2, 2, 2, 1, 1)
+S_COLS = (72, 72, 0, 40, 56, 56, 56, 56, 100, 100, 168, 72, 72)
+G_COLS = (0, 0, 0, 0, 48, 48, 48, 48, 48, 0, 0, 24, 24)
+C0_ON_VECTOR = 12
+PLANES_HEAD = 6
+PLANES_STEP = (6, 6, 5, 5, 5, 5, 5, 5, 5, 5)
+X_ON_VECTOR = ()
+IL_BUFS = 2
+EVAC_LAG = 2
+TAIL_FROM = 8
 
 
 def tile_autoreggqaattention_pa_kernel(
@@ -42,18 +47,17 @@ def tile_autoreggqaattention_pa_kernel(
     with ExitStack() as ctx:
         const = ctx.enter_context(tc.tile_pool(name="const", bufs=1))
         tmp = ctx.enter_context(tc.tile_pool(name="tmp", bufs=1))
-        xin = ctx.enter_context(tc.tile_pool(name="xin", bufs=1))
+        big = ctx.enter_context(tc.tile_pool(name="big", bufs=5))
+        small = ctx.enter_context(tc.tile_pool(name="small", bufs=8))
         wbp = ctx.enter_context(tc.tile_pool(name="wbp", bufs=1))
         rawp = ctx.enter_context(tc.tile_pool(name="rawp", bufs=1))
         widep = ctx.enter_context(tc.tile_pool(name="widep", bufs=3))
-        ilp = ctx.enter_context(tc.tile_pool(name="ilp", bufs=2))
+        ilp = ctx.enter_context(tc.tile_pool(name="ilp", bufs=IL_BUFS))
         cod = ctx.enter_context(tc.tile_pool(name="cod", bufs=4))
-        xgp = ctx.enter_context(tc.tile_pool(name="xgp", bufs=4))
         keep = ctx.enter_context(tc.tile_pool(name="keep", bufs=1))
-        ep = ctx.enter_context(tc.tile_pool(name="ep", bufs=3))
-        outp = ctx.enter_context(tc.tile_pool(name="outp", bufs=4))
         ps_acc = ctx.enter_context(tc.psum_pool(name="ps_acc", bufs=4))
         ps_tr = ctx.enter_context(tc.psum_pool(name="ps_tr", bufs=4))
+        ctx.enter_context(tc.manual_schedule())
 
         wscale = const.tile([P, PASSES, PACK], F32, name="wscale")
         nc.sync.dma_start(
@@ -67,13 +71,13 @@ def tile_autoreggqaattention_pa_kernel(
 
         wb = []
         for c in range(4):
-            wb_c = wbp.tile([P, PASSES * PACK, CH], U8, name="wb%d" % c, tag="wb%d" % c)
+            wb_c = wbp.tile([P, PLANES, CH], U8, name="wb%d" % c, tag="wb%d" % c)
             wb.append(wb_c)
-        raw_k = rawp.tile([P, PASSES * PACK, CH], BF16, name="raw_k", tag="raw_k")
-        raw_v = rawp.tile([P, PASSES * PACK, CH], BF16, name="raw_v", tag="raw_v")
+        raw_k = rawp.tile([P, PLANES, CH], BF16, name="raw_k", tag="raw_k")
+        raw_v = rawp.tile([P, PLANES, CH], BF16, name="raw_v", tag="raw_v")
         x_sb = []
         for a in range(4):
-            x_a = xin.tile([P, HID], BF16, name="x%d" % a, tag="x%d" % a)
+            x_a = big.tile([P, HID], BF16, name="x_a", tag="big")
             x_sb.append(x_a)
 
         def load_q(c):
@@ -89,10 +93,11 @@ def tile_autoreggqaattention_pa_kernel(
 
         brow = const.tile([P, P], BF16, name="brow")
         nc.vector.memset(brow[:], 0.0)
+        zero1 = const.tile([P, 1], F32, name="zero1")
+        nc.vector.memset(zero1[:], 0.0)
         load_q(0)
         nc.sync.dma_start(out=brow[0:16, :], in_=bq.rearrange("(h f) -> h f", f=DH))
         nc.sync.dma_start(out=brow[16:20, :], in_=bk.rearrange("(h f) -> h f", f=DH))
-        nc.sync.dma_start(out=brow[20:24, :], in_=bv.rearrange("(h f) -> h f", f=DH))
         for a in range(4):
             nc.sync.dma_start(out=x_sb[a][:], in_=hs[a])
         load_q(1)
@@ -100,20 +105,11 @@ def tile_autoreggqaattention_pa_kernel(
         load_q(2)
         load_kv(raw_v, wv_view)
         load_q(3)
+        bv_all = const.tile([P, 4 * DH], BF16, name="bv_all")
+        nc.sync.dma_start(out=bv_all[:], in_=bv.partition_broadcast(P))
 
-        zero1 = const.tile([P, 1], F32, name="zero1")
-        nc.vector.memset(zero1[:], 0.0)
         warm = const.tile([P, 1], F32, name="warm")
         nc.scalar.activation(out=warm[:], in_=zero1[:], func=ACT.Sin)
-
-        ident = const.tile([P, P], F32, name="ident")
-        make_identity(nc, ident[:])
-        ident_bf = const.tile([P, P], BF16, name="ident_bf")
-        make_identity(nc, ident_bf[:])
-        swap = const.tile([P, P], F32, name="swap")
-        nc.gpsimd.tensor_copy(out=swap[:, 0:64], in_=ident[:, 64:128])
-        nc.gpsimd.tensor_copy(out=swap[:, 64:128], in_=ident[:, 0:64])
-
         pidx = tmp.tile([P, 7], I32, name="pidx")
         nc.gpsimd.iota(pidx[:], pattern=[[0, 7]], base=0, channel_multiplier=1)
         shft = tmp.tile([P, 7], I32, name="shft")
@@ -126,6 +122,14 @@ def tile_autoreggqaattention_pa_kernel(
             channel_multiplier=0,
             allow_small_or_imprecise_dtypes=True,
         )
+        ident_bf = const.tile([P, P], BF16, name="ident_bf")
+        make_identity(nc, ident_bf[:])
+        ident = const.tile([P, P], F32, name="ident")
+        make_identity(nc, ident[:])
+        swap = const.tile([P, P], F32, name="swap")
+        nc.gpsimd.tensor_copy(out=swap[:, 0:64], in_=ident[:, 64:128])
+        nc.gpsimd.tensor_copy(out=swap[:, 64:128], in_=ident[:, 0:64])
+
         bsh = tmp.tile([P, 7], I32, name="bsh")
         nc.vector.tensor_tensor(out=bsh[:], in0=pidx[:], in1=shft[:], op=ALU.logical_shift_right)
         bit_i = tmp.tile([P, 7], I32, name="bit_i")
@@ -160,11 +164,10 @@ def tile_autoreggqaattention_pa_kernel(
         nc.vector.tensor_scalar(
             out=sgn2[:], in0=bit[:, 6:7], scalar1=-4.0, scalar2=2.0, op0=ALU.mult, op1=ALU.add
         )
-
         n_i = tmp.tile([P, TOK], I32, name="n_i")
         nc.vector.tensor_scalar(out=n_i[:], in0=tok[:], scalar1=turns[:], scalar2=None, op0=ALU.mult)
         ang = tmp.tile([P, TOK], F32, name="ang")
-        nc.scalar.activation(out=ang[:], in_=tok[:], func=ACT.Copy, scale=freq[:])
+        nc.vector.tensor_scalar(out=ang[:], in0=tok[:], scalar1=freq[:], scalar2=None, op0=ALU.mult)
         r1 = tmp.tile([P, TOK], F32, name="r1")
         nc.vector.scalar_tensor_tensor(
             out=r1[:], in0=n_i[:], scalar=-TWO_PI_HI, in1=ang[:], op0=ALU.mult, op1=ALU.add
@@ -173,185 +176,199 @@ def tile_autoreggqaattention_pa_kernel(
         nc.vector.scalar_tensor_tensor(
             out=red[:], in0=n_i[:], scalar=-TWO_PI_LO, in1=r1[:], op0=ALU.mult, op1=ALU.add
         )
+        ared = tmp.tile([P, TOK], F32, name="ared", tag="ang")
+        nc.scalar.activation(out=ared[:], in_=red[:], func=ACT.Abs)
+        s_h = tmp.tile([P, TOK], F32, name="s_h", tag="n_i")
+        nc.scalar.activation(out=s_h[:], in_=red[:], func=ACT.Sin, scale=0.5)
+        c_h = tmp.tile([P, TOK], F32, name="c_h", tag="tok")
+        nc.scalar.activation(out=c_h[:], in_=ared[:], func=ACT.Sin, scale=-0.5, bias=math.pi / 2.0)
+        cs = const.tile([P, 2, TOK], F32, name="cs")
+
+        def tables_vector():
+            nc.vector.scalar_tensor_tensor(
+                out=cs[:, 1, :], in0=s_h[:], scalar=sgn2[:], in1=c_h[:], op0=ALU.mult, op1=ALU.mult
+            )
+            sq = tmp.tile([P, TOK], F32, name="sq", tag="r1")
+            nc.vector.tensor_tensor(out=sq[:], in0=s_h[:], in1=s_h[:], op=ALU.mult)
+            nc.vector.tensor_scalar(
+                out=cs[:, 0, :], in0=sq[:], scalar1=-2.0, scalar2=1.0, op0=ALU.mult, op1=ALU.add
+            )
+
         wide = {}
 
-        def widen(c, g, t, lo, hi, on_vector):
+        def widen(c, k, on_vector):
             if c not in wide:
-                wide_c = widep.tile([P, PASSES * PACK, CH], BF16, name="wide", tag="wide")
+                wide_c = widep.tile([P, PLANES, CH], BF16, name="wide", tag="wide")
                 wide[c] = wide_c
-            k = PACK * g + t
+            scale_k = wscale[:, k // PACK, k % PACK : k % PACK + 1]
             if on_vector:
                 nc.vector.tensor_scalar(
-                    out=wide[c][:, k, lo:hi],
-                    in0=wb[c][:, k, lo:hi].bitcast(FP8),
-                    scalar1=wscale[:, g, t : t + 1],
+                    out=wide[c][:, k, :],
+                    in0=wb[c][:, k, :].bitcast(FP8),
+                    scalar1=scale_k,
                     scalar2=None,
                     op0=ALU.mult,
                 )
             else:
                 nc.scalar.activation(
-                    out=wide[c][:, k, lo:hi],
-                    in_=wb[c][:, k, lo:hi].bitcast(FP8),
-                    func=ACT.Copy,
-                    scale=wscale[:, g, t : t + 1],
+                    out=wide[c][:, k, :], in_=wb[c][:, k, :].bitcast(FP8), func=ACT.Copy, scale=scale_k
                 )
 
-        def widen_head(hh, on_vector):
-            for g in range(PASSES):
-                for t in range(PACK):
-                    widen(0, g, t, hh * DH, (hh + 1) * DH, on_vector)
+        pending = [(c, k) for c in (1, 2, 3) for k in range(PLANES)]
 
-        pending = [(c, g, t) for c in (1, 2, 3) for g in range(PASSES) for t in range(PACK)]
-        widen_head(0, True)
-        widen_head(1, False)
-
-        ared = tmp.tile([P, TOK], F32, name="ared")
-        nc.scalar.activation(out=ared[:], in_=red[:], func=ACT.Abs)
-        s_h = tmp.tile([P, TOK], F32, name="s_h")
-        nc.scalar.activation(out=s_h[:], in_=red[:], func=ACT.Sin, scale=0.5)
-        c_h = tmp.tile([P, TOK], F32, name="c_h")
-        nc.scalar.activation(out=c_h[:], in_=ared[:], func=ACT.Sin, scale=-0.5, bias=math.pi / 2.0)
-        stab = const.tile([P, TOK], F32, name="stab")
-        nc.vector.scalar_tensor_tensor(
-            out=stab[:], in0=s_h[:], scalar=sgn2[:], in1=c_h[:], op0=ALU.mult, op1=ALU.mult
-        )
-        sq = tmp.tile([P, TOK], F32, name="sq")
-        nc.vector.tensor_tensor(out=sq[:], in0=s_h[:], in1=s_h[:], op=ALU.mult)
-        ctab = const.tile([P, TOK], F32, name="ctab")
-        nc.vector.tensor_scalar(
-            out=ctab[:], in0=sq[:], scalar1=-2.0, scalar2=1.0, op0=ALU.mult, op1=ALU.add
-        )
-
-        widen_head(2, False)
-        widen_head(3, False)
-
-        bias_ps = ps_tr.tile([P, P], BF16, name="bias_ps", tag="tr")
-        nc.tensor.transpose(bias_ps[:], brow[:], ident_bf[:])
-        bias = const.tile([P, 24], F32, name="bias")
-        nc.vector.tensor_copy(out=bias[:], in_=bias_ps[:, 0:24])
+        def planes(count):
+            for c, k in pending[0:count]:
+                widen(c, k, False)
+                pending.remove((c, k))
 
         xc = keep.tile([P, PASSES, TOK], U32, name="xc", align_bytes=64)
         xs = keep.tile([P, PASSES, TOK], U8, name="xs", align_bytes=64)
-        for jp in range(2):
-            banks = []
+        banks = {}
+        grouped = {}
+
+        def x_transposes(jp):
             for g in range(PASSES):
-                xt = ps_tr.tile([P, 2, 256], F32, name="xt", tag="tr")
-                banks.append(xt)
+                if jp == 0:
+                    xt = ps_tr.tile([P, 2, 256], F32, name="xt", tag="tr")
+                else:
+                    xt = ps_acc.tile([P, 2, 256], F32, name="xt", tag="acc")
+                banks[(jp, g)] = xt
             for al in range(2):
                 words = x_sb[2 * jp + al][:].bitcast(F32)
                 for g in range(PASSES):
                     for u in range(2):
                         nc.tensor.transpose(
-                            banks[g][:, u, al * P : (al + 1) * P],
+                            banks[(jp, g)][:, u, al * P : (al + 1) * P],
                             words[:, 256 * g + u : 256 * (g + 1) : 2],
                             ident[:],
                         )
-            grouped = []
-            for step in range(PASSES + 1):
-                if step < PASSES:
-                    g = step
-                    xg = xgp.tile([P, 256, PACK], BF16, name="xg", tag="xg", align_bytes=64)
-                    grouped.append(xg)
-                    xg_words = xg[:].rearrange("p r t -> p (r t)").bitcast(F32).rearrange("p (r u) -> p r u", u=2)
-                    if jp == 1 and g % 2 == 1:
-                        nc.scalar.copy(out=xg_words, in_=banks[g][:].rearrange("p u r -> p r u"))
-                    else:
-                        nc.vector.tensor_copy(out=xg_words, in_=banks[g][:].rearrange("p u r -> p r u"))
-                if step > 0:
-                    g = step - 1
-                    cols = slice(jp * 256, (jp + 1) * 256)
-                    nc.vector.quantize_mx(
-                        out=xc[:, g, cols].bitcast(FP8X4),
-                        scales=xs[:, g, cols],
-                        in_=grouped[g][:].rearrange("p r t -> p (r t)"),
-                    )
+
+        def x_empty(jp, g):
+            xg = small.tile([P, 256, PACK], BF16, name="xg", tag="small", align_bytes=64)
+            grouped[(jp, g)] = xg
+            xg_words = xg[:].rearrange("p r t -> p (r t)").bitcast(F32).rearrange("p (r u) -> p r u", u=2)
+            if (jp, g) in X_ON_VECTOR:
+                nc.vector.tensor_copy(out=xg_words, in_=banks[(jp, g)][:].rearrange("p u r -> p r u"))
+            else:
+                nc.scalar.copy(out=xg_words, in_=banks[(jp, g)][:].rearrange("p u r -> p r u"))
+
+        def x_quant(jp, g):
+            cols = slice(jp * 256, (jp + 1) * 256)
+            nc.vector.quantize_mx(
+                out=xc[:, g, cols].bitcast(FP8X4),
+                scales=xs[:, g, cols],
+                in_=grouped[(jp, g)][:].rearrange("p r t -> p (r t)"),
+            )
 
         oq = out_0[0].rearrange("h (p a) f -> h p (a f)", a=4)
         ok = out_1[0].rearrange("h (p a) f -> h p (a f)", a=4)
-        ov = out_2[0].rearrange("h (p a) f -> h p (a f)", a=4)
+        ov = out_2[0].rearrange("(w hh) (p b a) f -> w b p hh (a f)", hh=2, b=2, a=2)
         heads = []
         for kind, c in (("q", 0), ("k", 0), ("q", 1), ("v", 0), ("q", 2), ("q", 3)):
             for hh in range(4):
                 heads.append((kind, c, hh))
-
         n_heads = len(heads)
+        units = []
+        unit_of = {}
+        for size in UNIT_SIZES:
+            first = sum([len(hs_u) for hs_u in units])
+            units.append(list(range(first, first + size)))
+            for j in units[-1]:
+                unit_of[j] = len(units) - 1
+        n_units = len(units)
+        assert sum(UNIT_SIZES) == n_heads
         state = {}
 
-        def source(j):
+        def weights(j):
             kind, c, hh = heads[j]
             if kind == "q":
-                return wide[c], 4 * c + hh, oq[4 * c + hh]
+                return wide[c]
             if kind == "k":
-                return raw_k, 16 + hh, ok[hh]
-            return raw_v, 20 + hh, ov[hh]
+                return raw_k
+            return raw_v
 
-        def n_gpsimd(j):
-            if j >= 3 and heads[j - 3][0] != "v":
-                return NG
-            return 0
+        def width(u):
+            return DH * len(units[u])
 
-        def n_vector(j):
-            if heads[j][0] == "v":
-                return NV_VALUE - n_gpsimd(j)
-            if j < 16:
-                return NV_EARLY - (2 * n_gpsimd(j)) // 3
-            return NV_LATE - n_gpsimd(j) // 2
+        def n_vector(u):
+            return width(u) - G_COLS[u] - S_COLS[u]
 
-        def il_tile(j):
-            if ("il", j) not in state:
-                il = ilp.tile([P, PASSES, DH, PACK], BF16, name="il", tag="il", align_bytes=64)
-                state[("il", j)] = il
-            return state[("il", j)]
+        def il_tile(u):
+            if ("il", u) not in state:
+                il = ilp.tile([P, PASSES, width(u), PACK], BF16, name="il", tag="il", align_bytes=64)
+                state[("il", u)] = il
+            return state[("il", u)]
 
-        def il_view(j, lo, hi):
-            src = source(j)[0]
-            hh = heads[j][2]
-            return src[:, :, hh * DH + lo : hh * DH + hi].rearrange("p (g t) (c i) -> p g c t i", t=PACK, i=4)
+        def columns(u, lo, hi):
+            j = units[u][0]
+            base_col = heads[j][2] * DH
+            return weights(j)[:, :, base_col + lo : base_col + hi]
 
-        def il_gpsimd(j):
-            lo = n_vector(j)
-            hi = lo + n_gpsimd(j)
+        def il_view(u, lo, hi):
+            return columns(u, lo, hi).rearrange("p (g t) (c i) -> p g c t i", t=PACK, i=4)
+
+        def il_gpsimd(u):
+            lo = n_vector(u)
+            hi = lo + G_COLS[u]
             if hi > lo:
-                src = source(j)[0]
-                hh = heads[j][2]
                 nc.gpsimd.tensor_scalar(
-                    out=il_tile(j)[:, :, lo:hi, :],
-                    in0=src[:, :, hh * DH + lo : hh * DH + hi].rearrange("p (g t) n -> p g n t", t=PACK),
+                    out=il_tile(u)[:, :, lo:hi, :],
+                    in0=columns(u, lo, hi).rearrange("p (g t) n -> p g n t", t=PACK),
                     scalar1=1.0,
                     scalar2=0.0,
                     op0=ALU.mult,
                     op1=ALU.add,
                 )
 
-        def il_scalar(j):
-            nv = n_vector(j) + n_gpsimd(j)
-            if nv < DH:
+        def il_scalar(u):
+            lo = width(u) - S_COLS[u]
+            if S_COLS[u] > 0:
                 nc.scalar.copy(
-                    out=il_tile(j)[:, :, nv:DH, :].rearrange("p g (c i) t -> p g c t i", i=4), in_=il_view(j, nv, DH)
+                    out=il_tile(u)[:, :, lo : width(u), :].rearrange("p g (c i) t -> p g c t i", i=4),
+                    in_=il_view(u, lo, width(u)),
                 )
 
-        def il_vector(j):
-            nv = n_vector(j)
-            nc.vector.tensor_copy(
-                out=il_tile(j)[:, :, 0:nv, :].rearrange("p g (c i) t -> p g c t i", i=4), in_=il_view(j, 0, nv)
-            )
+        def il_vector(u):
+            nv = n_vector(u)
+            if nv > 0:
+                nc.vector.tensor_copy(
+                    out=il_tile(u)[:, :, 0:nv, :].rearrange("p g (c i) t -> p g c t i", i=4), in_=il_view(u, 0, nv)
+                )
 
-        def quant(j):
-            wc = cod.tile([P, PASSES * DH], U32, name="wc", tag="wc", align_bytes=64)
-            ws = cod.tile([P, PASSES * DH], U8, name="ws", tag="ws", align_bytes=64)
+        def quant(u):
+            wc = cod.tile([P, PASSES * width(u)], U32, name="wc", tag="wc", align_bytes=64)
+            ws = cod.tile([P, PASSES * width(u)], U8, name="ws", tag="ws", align_bytes=64)
             nc.vector.quantize_mx(
                 out=wc[:].bitcast(FP8X4),
                 scales=ws[:],
-                in_=il_tile(j)[:].rearrange("p g n t -> p (g n t)"),
+                in_=il_tile(u)[:].rearrange("p g n t -> p (g n t)"),
             )
-            state[("wc", j)] = wc
-            state[("ws", j)] = ws
+            state[("wc", u)] = wc
+            state[("ws", u)] = ws
 
         def mx(j):
+            u = unit_of[j]
+            place = j - units[u][0]
             acc = ps_acc.tile([P, TOK], F32, name="acc", tag="acc")
-            wc, ws = state[("wc", j)], state[("ws", j)]
+            wc, ws = state[("wc", u)], state[("ws", u)]
+            state[("acc", j)] = acc
+            if heads[j][0] == "v":
+                for a in range(2):
+                    blk = slice((2 * place + a) * P, (2 * place + a + 1) * P)
+                    for g in range(PASSES):
+                        cols = slice(g * width(u), (g + 1) * width(u))
+                        nc.tensor.matmul_mx(
+                            out=acc[:, a * 2 * DH : (a + 1) * 2 * DH],
+                            lhsT=xc[:, g, blk].bitcast(FP8X4),
+                            lhsT_scale=xs[:, g, blk],
+                            rhs=wc[:, cols].bitcast(FP8X4),
+                            rhs_scale=ws[:, cols],
+                            start=(g == 0),
+                            stop=(g == PASSES - 1),
+                        )
+                return
             for g in range(PASSES):
-                cols = slice(g * DH, (g + 1) * DH)
+                cols = slice(g * width(u) + place * DH, g * width(u) + (place + 1) * DH)
                 nc.tensor.matmul_mx(
                     out=acc[:],
                     lhsT=wc[:, cols].bitcast(FP8X4),
@@ -361,76 +378,112 @@ def tile_autoreggqaattention_pa_kernel(
                     start=(g == 0),
                     stop=(g == PASSES - 1),
                 )
-            state[("acc", j)] = acc
 
         def rope(j):
+            kind, c, hh = heads[j]
             acc = state[("acc", j)]
-            bcol = source(j)[1]
-            b_ap = bias[:, bcol : bcol + 1]
-            u_t = ep.tile([P, TOK], F32, name="u_t", tag="u_t")
-            state[("u", j)] = u_t
-            if heads[j][0] == "v":
-                nc.vector.tensor_scalar(out=u_t[:], in0=acc[:], scalar1=b_ap, scalar2=None, op0=ALU.add)
+            if kind == "v":
+                first_col = (hh // 2) * 2 * DH
+                ob = small.tile([P, 2, 2, DH], F32, name="ob", tag="small", align_bytes=64)
+                nc.vector.tensor_tensor(
+                    out=ob[:].rearrange("p hh a f -> p a hh f"),
+                    in0=acc[:].rearrange("p (a hh f) -> p a hh f", a=2, hh=2),
+                    in1=bv_all[:, first_col : first_col + 2 * DH]
+                    .rearrange("p (hh f) -> p hh f", hh=2)
+                    .unsqueeze(1)
+                    .to_broadcast([P, 2, 2, DH]),
+                    op=ALU.add,
+                )
+                nc.sync.dma_start(out=ov[hh // 2][hh % 2], in_=ob[:].rearrange("p hh a f -> p hh (a f)"))
                 return
-            w_t = ep.tile([P, TOK], F32, name="w_t", tag="w_t")
-            state[("w", j)] = w_t
+            bcol = 4 * c + hh if kind == "q" else 16 + hh
+            uw = big.tile([P, 2, TOK], F32, name="uw", tag="big")
+            state[("uw", j)] = uw
             nc.vector.scalar_tensor_tensor(
-                out=u_t[:], in0=acc[:], scalar=b_ap, in1=ctab[:], op0=ALU.add, op1=ALU.mult
-            )
-            nc.vector.scalar_tensor_tensor(
-                out=w_t[:], in0=acc[:], scalar=b_ap, in1=stab[:], op0=ALU.add, op1=ALU.mult
+                out=uw[:],
+                in0=acc[:].unsqueeze(1).to_broadcast([P, 2, TOK]),
+                scalar=bias[:, bcol : bcol + 1],
+                in1=cs[:],
+                op0=ALU.add,
+                op1=ALU.mult,
             )
 
         def tback(j):
+            if heads[j][0] == "v":
+                return
             tr = ps_tr.tile([P, TOK], F32, name="tr", tag="tr")
             state[("tr", j)] = tr
-            u_t = state[("u", j)]
+            uw = state[("uw", j)]
             for a in range(4):
                 blk = slice(a * P, (a + 1) * P)
-                if heads[j][0] == "v":
-                    nc.tensor.transpose(tr[:, blk], u_t[:, blk], ident[:])
-                else:
-                    w_t = state[("w", j)]
-                    nc.tensor.matmul(
-                        tr[:, blk], lhsT=u_t[:, blk], rhs=ident[:], start=True, stop=False, is_transpose=True
-                    )
-                    nc.tensor.matmul(
-                        tr[:, blk], lhsT=w_t[:, blk], rhs=swap[:], start=False, stop=True, is_transpose=True
-                    )
+                nc.tensor.matmul(
+                    tr[:, blk], lhsT=uw[:, 0, blk], rhs=ident[:], start=True, stop=False, is_transpose=True
+                )
+                nc.tensor.matmul(
+                    tr[:, blk], lhsT=uw[:, 1, blk], rhs=swap[:], start=False, stop=True, is_transpose=True
+                )
 
         def evac(j):
-            ob = outp.tile([P, TOK], F32, name="ob", tag="ob")
+            kind, c, hh = heads[j]
+            if kind == "v":
+                return
+            ob = small.tile([P, TOK], F32, name="ob", tag="small", align_bytes=64)
             nc.scalar.copy(out=ob[:], in_=state[("tr", j)][:])
-            nc.sync.dma_start(out=source(j)[2], in_=ob[:])
+            nc.sync.dma_start(out=oq[4 * c + hh] if kind == "q" else ok[hh], in_=ob[:])
 
-        def live(j):
-            return 0 <= j < n_heads
+        def members(u):
+            if 0 <= u < n_units:
+                return units[u]
+            return []
 
-        if MANUAL:
-            ctx.enter_context(tc.manual_schedule())
-        next_plane = 0
+        for k in range(PLANES):
+            widen(0, k, k < C0_ON_VECTOR)
+        x_transposes(0)
+        x_transposes(1)
+        tables_vector()
         il_scalar(0)
-        for i in range(-2, n_heads + 2):
-            if live(i - 1) and i < n_heads - 3:
-                tback(i - 1)
-            if live(i + 1):
-                mx(i + 1)
-            if live(i - 1) and i >= n_heads - 3:
-                tback(i - 1)
-            if live(i + 3):
-                il_gpsimd(i + 3)
-            if live(i + 2):
+        il_vector(0)
+        for g in range(PASSES):
+            x_empty(0, g)
+        quant(0)
+        il_scalar(1)
+        for g in range(PASSES):
+            x_quant(0, g)
+        for g in range(PASSES):
+            x_empty(1, g)
+        il_vector(1)
+        planes(PLANES_HEAD)
+        for g in range(PASSES):
+            x_quant(1, g)
+        bias_ps = ps_tr.tile([P, P], BF16, name="bias_ps", tag="tr")
+        nc.tensor.transpose(bias_ps[:], brow[:], ident_bf[:])
+        bias = const.tile([P, 20], F32, name="bias")
+        nc.vector.tensor_copy(out=bias[:], in_=bias_ps[:, 0:20])
+        quant(1)
+        il_scalar(2)
+        for i in range(-1, n_units + 1 + EVAC_LAG):
+            back, ahead = members(i - 1), members(i + 1)
+            if i < TAIL_FROM:
+                for k in range(2):
+                    for j in back[k : k + 1]:
+                        tback(j)
+                    for j in ahead[k : k + 1]:
+                        mx(j)
+            else:
+                for j in back:
+                    tback(j)
+                for j in ahead:
+                    mx(j)
+            if members(i + 2) and i >= 0:
                 il_vector(i + 2)
-            if live(i):
-                rope(i)
-            if live(i + 2):
+            for j in members(i):
+                rope(j)
+            if members(i + 2) and i >= 0:
                 quant(i + 2)
-            for j in range(PLANES_PER_SLOT):
-                if next_plane < len(pending):
-                    pc, pg, pt = pending[next_plane]
-                    next_plane += 1
-                    widen(pc, pg, pt, 0, CH, False)
-            if live(i + 3):
+            if 0 <= i + 1 < len(PLANES_STEP):
+                planes(PLANES_STEP[i + 1])
+            if members(i + 3):
+                il_gpsimd(i + 3)
                 il_scalar(i + 3)
-            if live(i - 1):
-                evac(i - 1)
+            for j in members(i - EVAC_LAG):
+                evac(j)

@@ -29,7 +29,7 @@ TWO_PI_HI = 6.28125
 TWO_PI_LO = 2.0 * math.pi - TWO_PI_HI
 
 UNIT_SIZES = (2, 2, 2, 2, 2, 2, 2, 2, 2, 2, 2, 1, 1)
-S_COLS = (72, 72, 0, 40, 56, 56, 56, 56, 100, 100, 168, 72, 72)
+S_COLS = (56, 64, 0, 32, 48, 48, 48, 48, 92, 92, 160, 72, 72)
 G_COLS = (0, 0, 0, 0, 48, 48, 48, 48, 48, 0, 0, 24, 24)
 C0_ON_VECTOR = 12
 PLANES_HEAD = 6
@@ -38,6 +38,8 @@ X_ON_VECTOR = ()
 IL_BUFS = 2
 EVAC_LAG = 2
 TAIL_FROM = 8
+MX_FIRST_FROM = 20
+FINE_HEADS = 1
 
 
 def tile_autoreggqaattention_pa_kernel(
@@ -48,7 +50,7 @@ def tile_autoreggqaattention_pa_kernel(
         const = ctx.enter_context(tc.tile_pool(name="const", bufs=1))
         tmp = ctx.enter_context(tc.tile_pool(name="tmp", bufs=1))
         big = ctx.enter_context(tc.tile_pool(name="big", bufs=5))
-        small = ctx.enter_context(tc.tile_pool(name="small", bufs=8))
+        small = ctx.enter_context(tc.tile_pool(name="small", bufs=6))
         wbp = ctx.enter_context(tc.tile_pool(name="wbp", bufs=1))
         rawp = ctx.enter_context(tc.tile_pool(name="rawp", bufs=1))
         widep = ctx.enter_context(tc.tile_pool(name="widep", bufs=3))
@@ -77,7 +79,7 @@ def tile_autoreggqaattention_pa_kernel(
         raw_v = rawp.tile([P, PLANES, CH], BF16, name="raw_v", tag="raw_v")
         x_sb = []
         for a in range(4):
-            x_a = big.tile([P, HID], BF16, name="x_a", tag="big")
+            x_a = big.tile([P, HID], BF16, name="x_a", tag="big", align_bytes=64)
             x_sb.append(x_a)
 
         def load_q(c):
@@ -160,9 +162,9 @@ def tile_autoreggqaattention_pa_kernel(
         nc.vector.tensor_scalar(
             out=turns[:], in0=freq[:], scalar1=1.0 / (2.0 * math.pi), scalar2=None, op0=ALU.mult
         )
-        sgn2 = tmp.tile([P, 1], F32, name="sgn2")
+        sgn = tmp.tile([P, 1], F32, name="sgn")
         nc.vector.tensor_scalar(
-            out=sgn2[:], in0=bit[:, 6:7], scalar1=-4.0, scalar2=2.0, op0=ALU.mult, op1=ALU.add
+            out=sgn[:], in0=bit[:, 6:7], scalar1=-2.0, scalar2=1.0, op0=ALU.mult, op1=ALU.add
         )
         n_i = tmp.tile([P, TOK], I32, name="n_i")
         nc.vector.tensor_scalar(out=n_i[:], in0=tok[:], scalar1=turns[:], scalar2=None, op0=ALU.mult)
@@ -176,23 +178,11 @@ def tile_autoreggqaattention_pa_kernel(
         nc.vector.scalar_tensor_tensor(
             out=red[:], in0=n_i[:], scalar=-TWO_PI_LO, in1=r1[:], op0=ALU.mult, op1=ALU.add
         )
+        cs = const.tile([P, 2, TOK], F32, name="cs")
         ared = tmp.tile([P, TOK], F32, name="ared", tag="ang")
         nc.scalar.activation(out=ared[:], in_=red[:], func=ACT.Abs)
-        s_h = tmp.tile([P, TOK], F32, name="s_h", tag="n_i")
-        nc.scalar.activation(out=s_h[:], in_=red[:], func=ACT.Sin, scale=0.5)
-        c_h = tmp.tile([P, TOK], F32, name="c_h", tag="tok")
-        nc.scalar.activation(out=c_h[:], in_=ared[:], func=ACT.Sin, scale=-0.5, bias=math.pi / 2.0)
-        cs = const.tile([P, 2, TOK], F32, name="cs")
-
-        def tables_vector():
-            nc.vector.scalar_tensor_tensor(
-                out=cs[:, 1, :], in0=s_h[:], scalar=sgn2[:], in1=c_h[:], op0=ALU.mult, op1=ALU.mult
-            )
-            sq = tmp.tile([P, TOK], F32, name="sq", tag="r1")
-            nc.vector.tensor_tensor(out=sq[:], in0=s_h[:], in1=s_h[:], op=ALU.mult)
-            nc.vector.tensor_scalar(
-                out=cs[:, 0, :], in0=sq[:], scalar1=-2.0, scalar2=1.0, op0=ALU.mult, op1=ALU.add
-            )
+        nc.scalar.activation(out=cs[:, 1, :], in_=red[:], func=ACT.Sin, scale=sgn[:])
+        nc.scalar.activation(out=cs[:, 0, :], in_=ared[:], func=ACT.Sin, scale=-1.0, bias=math.pi / 2.0)
 
         wide = {}
 
@@ -244,20 +234,21 @@ def tile_autoreggqaattention_pa_kernel(
                         )
 
         def x_empty(jp, g):
-            xg = small.tile([P, 256, PACK], BF16, name="xg", tag="small", align_bytes=64)
-            grouped[(jp, g)] = xg
-            xg_words = xg[:].rearrange("p r t -> p (r t)").bitcast(F32).rearrange("p (r u) -> p r u", u=2)
+            if g not in grouped:
+                xg = big.tile([P, TOK, PACK], BF16, name="xg", tag="big", align_bytes=64)
+                grouped[g] = xg
+            half = grouped[g][:, jp * 256 : (jp + 1) * 256, :]
+            xg_words = half.rearrange("p r t -> p (r t)").bitcast(F32).rearrange("p (r u) -> p r u", u=2)
             if (jp, g) in X_ON_VECTOR:
                 nc.vector.tensor_copy(out=xg_words, in_=banks[(jp, g)][:].rearrange("p u r -> p r u"))
             else:
                 nc.scalar.copy(out=xg_words, in_=banks[(jp, g)][:].rearrange("p u r -> p r u"))
 
-        def x_quant(jp, g):
-            cols = slice(jp * 256, (jp + 1) * 256)
+        def x_quant(g):
             nc.vector.quantize_mx(
-                out=xc[:, g, cols].bitcast(FP8X4),
-                scales=xs[:, g, cols],
-                in_=grouped[(jp, g)][:].rearrange("p r t -> p (r t)"),
+                out=xc[:, g, :].bitcast(FP8X4),
+                scales=xs[:, g, :],
+                in_=grouped[g][:].rearrange("p r t -> p (r t)"),
             )
 
         oq = out_0[0].rearrange("h (p a) f -> h p (a f)", a=4)
@@ -346,6 +337,11 @@ def tile_autoreggqaattention_pa_kernel(
             state[("wc", u)] = wc
             state[("ws", u)] = ws
 
+        def pieces(j):
+            if j >= n_heads - FINE_HEADS:
+                return [slice(0, TOK // 2), slice(TOK // 2, TOK)]
+            return [slice(0, TOK)]
+
         def mx(j):
             u = unit_of[j]
             place = j - units[u][0]
@@ -397,16 +393,17 @@ def tile_autoreggqaattention_pa_kernel(
                 nc.sync.dma_start(out=ov[hh // 2][hh % 2], in_=ob[:].rearrange("p hh a f -> p hh (a f)"))
                 return
             bcol = 4 * c + hh if kind == "q" else 16 + hh
-            uw = big.tile([P, 2, TOK], F32, name="uw", tag="big")
+            uw = big.tile([P, 2, TOK], F32, name="uw", tag="big", align_bytes=64)
             state[("uw", j)] = uw
-            nc.vector.scalar_tensor_tensor(
-                out=uw[:],
-                in0=acc[:].unsqueeze(1).to_broadcast([P, 2, TOK]),
-                scalar=bias[:, bcol : bcol + 1],
-                in1=cs[:],
-                op0=ALU.add,
-                op1=ALU.mult,
-            )
+            for cols in pieces(j):
+                nc.vector.scalar_tensor_tensor(
+                    out=uw[:, :, cols],
+                    in0=acc[:, cols].unsqueeze(1).to_broadcast([P, 2, cols.stop - cols.start]),
+                    scalar=bias[:, bcol : bcol + 1],
+                    in1=cs[:, :, cols],
+                    op0=ALU.add,
+                    op1=ALU.mult,
+                )
 
         def tback(j):
             if heads[j][0] == "v":
@@ -428,8 +425,9 @@ def tile_autoreggqaattention_pa_kernel(
             if kind == "v":
                 return
             ob = small.tile([P, TOK], F32, name="ob", tag="small", align_bytes=64)
-            nc.scalar.copy(out=ob[:], in_=state[("tr", j)][:])
-            nc.sync.dma_start(out=oq[4 * c + hh] if kind == "q" else ok[hh], in_=ob[:])
+            for cols in pieces(j):
+                nc.scalar.copy(out=ob[:, cols], in_=state[("tr", j)][:, cols])
+                nc.sync.dma_start(out=(oq[4 * c + hh] if kind == "q" else ok[hh])[:, cols], in_=ob[:, cols])
 
         def members(u):
             if 0 <= u < n_units:
@@ -440,21 +438,18 @@ def tile_autoreggqaattention_pa_kernel(
             widen(0, k, k < C0_ON_VECTOR)
         x_transposes(0)
         x_transposes(1)
-        tables_vector()
         il_scalar(0)
         il_vector(0)
         for g in range(PASSES):
             x_empty(0, g)
         quant(0)
-        il_scalar(1)
-        for g in range(PASSES):
-            x_quant(0, g)
         for g in range(PASSES):
             x_empty(1, g)
+        il_scalar(1)
         il_vector(1)
         planes(PLANES_HEAD)
         for g in range(PASSES):
-            x_quant(1, g)
+            x_quant(g)
         bias_ps = ps_tr.tile([P, P], BF16, name="bias_ps", tag="tr")
         nc.tensor.transpose(bias_ps[:], brow[:], ident_bf[:])
         bias = const.tile([P, 20], F32, name="bias")
@@ -469,11 +464,16 @@ def tile_autoreggqaattention_pa_kernel(
                         tback(j)
                     for j in ahead[k : k + 1]:
                         mx(j)
-            else:
+            elif i < MX_FIRST_FROM:
                 for j in back:
                     tback(j)
                 for j in ahead:
                     mx(j)
+            else:
+                for j in ahead:
+                    mx(j)
+                for j in back:
+                    tback(j)
             if members(i + 2) and i >= 0:
                 il_vector(i + 2)
             for j in members(i):

@@ -29,8 +29,8 @@ TWO_PI_HI = 6.28125
 TWO_PI_LO = 2.0 * math.pi - TWO_PI_HI
 
 UNIT_SIZES = (2, 2, 2, 2, 2, 2, 2, 2, 2, 2, 2, 1, 1)
-S_COLS = (56, 64, 0, 32, 48, 48, 48, 48, 92, 92, 160, 72, 72)
-G_COLS = (0, 0, 0, 0, 48, 48, 48, 48, 48, 0, 0, 24, 24)
+S_COLS = (56, 64, 0, 32, 32, 32, 32, 32, 76, 92, 160, 60, 60)
+G_COLS = (0, 0, 0, 0, 96, 96, 96, 96, 96, 0, 0, 48, 48)
 C0_ON_VECTOR = 12
 PLANES_HEAD = 6
 PLANES_STEP = (6, 6, 5, 5, 5, 5, 5, 5, 5, 5)

@@ -29,8 +29,8 @@ TWO_PI_HI = 6.28125
 TWO_PI_LO = 2.0 * math.pi - TWO_PI_HI
 
 UNIT_SIZES = (2, 2, 2, 2, 2, 2, 2, 2, 2, 2, 2, 1, 1)
-S_COLS = (56, 64, 0, 32, 32, 32, 32, 32, 76, 92, 160, 60, 60)
-G_COLS = (0, 0, 0, 0, 96, 96, 96, 96, 96, 0, 0, 48, 48)
+S_COLS = (56, 64, 0, 16, 32, 32, 32, 32, 76, 76, 140, 32, 32)
+G_COLS = (0, 0, 0, 96, 96, 96, 96, 96, 96, 48, 48, 96, 96)
 C0_ON_VECTOR = 12
 PLANES_HEAD = 6
 PLANES_STEP = (6, 6, 5, 5, 5, 5, 5, 5, 5, 5)

@@ -29,9 +29,11 @@ TWO_PI_HI = 6.28125
 TWO_PI_LO = 2.0 * math.pi - TWO_PI_HI
 
 UNIT_SIZES = (2, 2, 2, 2, 2, 2, 2, 2, 2, 2, 2, 1, 1)
-S_COLS = (56, 64, 0, 16, 32, 32, 32, 32, 76, 76, 140, 32, 32)
+S_COLS = (0, 0, 0, 16, 48, 48, 48, 48, 92, 92, 160, 32, 32)
 G_COLS = (0, 0, 0, 96, 96, 96, 96, 96, 96, 48, 48, 96, 96)
-C0_ON_VECTOR = 12
+C0_ON_SCALAR = (0, 1, 2, 3, 4, 5, 12, 13, 14, 15)
+TABLES_AT = 3
+IL1_EARLY = False
 PLANES_HEAD = 6
 PLANES_STEP = (6, 6, 5, 5, 5, 5, 5, 5, 5, 5)
 X_ON_VECTOR = ()
@@ -40,6 +42,9 @@ EVAC_LAG = 2
 TAIL_FROM = 8
 MX_FIRST_FROM = 20
 FINE_HEADS = 1
+LOAD_ORDER = (0, "b", "x", 1, "k", 2, "v", 3)
+ORDER = (("q", 0), ("k", 0), ("q", 1), ("v", 0), ("q", 2), ("q", 3))
+PLANES_STEP_V = (0, 0, 0, 0, 0, 0, 0, 0, 0, 0)
 
 
 def tile_autoreggqaattention_pa_kernel(
@@ -72,8 +77,8 @@ def tile_autoreggqaattention_pa_kernel(
         hs = hidden_states[0].rearrange("(p a) h -> a p h", a=4)
 
         wb = []
-        for c in range(4):
-            wb_c = wbp.tile([P, PLANES, CH], U8, name="wb%d" % c, tag="wb%d" % c)
+        for c in range(2):
+            wb_c = wbp.tile([P, PLANES, 2 * CH], U8, name="wb%d" % c, tag="wb%d" % c)
             wb.append(wb_c)
         raw_k = rawp.tile([P, PLANES, CH], BF16, name="raw_k", tag="raw_k")
         raw_v = rawp.tile([P, PLANES, CH], BF16, name="raw_v", tag="raw_v")
@@ -83,10 +88,11 @@ def tile_autoreggqaattention_pa_kernel(
             x_sb.append(x_a)
 
         def load_q(c):
+            lo, hi = (c * CH, (c + 1) * CH) if c < 4 else ((c - 4) * 2 * CH, (c - 3) * 2 * CH)
             for g in range(PASSES):
                 nc.sync.dma_start(
-                    out=wb[c][:, PACK * g : PACK * (g + 1), :],
-                    in_=wq_view[g][:, :, c * CH : (c + 1) * CH],
+                    out=wb[lo // (2 * CH)][:, PACK * g : PACK * (g + 1), lo % (2 * CH) : lo % (2 * CH) + hi - lo],
+                    in_=wq_view[g][:, :, lo:hi],
                 )
 
         def load_kv(dst, view):
@@ -97,16 +103,19 @@ def tile_autoreggqaattention_pa_kernel(
         nc.vector.memset(brow[:], 0.0)
         zero1 = const.tile([P, 1], F32, name="zero1")
         nc.vector.memset(zero1[:], 0.0)
-        load_q(0)
-        nc.sync.dma_start(out=brow[0:16, :], in_=bq.rearrange("(h f) -> h f", f=DH))
-        nc.sync.dma_start(out=brow[16:20, :], in_=bk.rearrange("(h f) -> h f", f=DH))
-        for a in range(4):
-            nc.sync.dma_start(out=x_sb[a][:], in_=hs[a])
-        load_q(1)
-        load_kv(raw_k, wk_view)
-        load_q(2)
-        load_kv(raw_v, wv_view)
-        load_q(3)
+        for what in LOAD_ORDER:
+            if what == "x":
+                for a in range(4):
+                    nc.sync.dma_start(out=x_sb[a][:], in_=hs[a])
+            elif what == "b":
+                nc.sync.dma_start(out=brow[0:16, :], in_=bq.rearrange("(h f) -> h f", f=DH))
+                nc.sync.dma_start(out=brow[16:20, :], in_=bk.rearrange("(h f) -> h f", f=DH))
+            elif what == "k":
+                load_kv(raw_k, wk_view)
+            elif what == "v":
+                load_kv(raw_v, wv_view)
+            else:
+                load_q(what)
         bv_all = const.tile([P, 4 * DH], BF16, name="bv_all")
         nc.sync.dma_start(out=bv_all[:], in_=bv.partition_broadcast(P))
 
@@ -170,19 +179,17 @@ def tile_autoreggqaattention_pa_kernel(
         nc.vector.tensor_scalar(out=n_i[:], in0=tok[:], scalar1=turns[:], scalar2=None, op0=ALU.mult)
         ang = tmp.tile([P, TOK], F32, name="ang")
         nc.vector.tensor_scalar(out=ang[:], in0=tok[:], scalar1=freq[:], scalar2=None, op0=ALU.mult)
-        r1 = tmp.tile([P, TOK], F32, name="r1")
-        nc.vector.scalar_tensor_tensor(
-            out=r1[:], in0=n_i[:], scalar=-TWO_PI_HI, in1=ang[:], op0=ALU.mult, op1=ALU.add
-        )
         red = tmp.tile([P, TOK], F32, name="red")
         nc.vector.scalar_tensor_tensor(
-            out=red[:], in0=n_i[:], scalar=-TWO_PI_LO, in1=r1[:], op0=ALU.mult, op1=ALU.add
+            out=red[:], in0=n_i[:], scalar=-2.0 * math.pi, in1=ang[:], op0=ALU.mult, op1=ALU.add
         )
         cs = const.tile([P, 2, TOK], F32, name="cs")
-        ared = tmp.tile([P, TOK], F32, name="ared", tag="ang")
-        nc.scalar.activation(out=ared[:], in_=red[:], func=ACT.Abs)
-        nc.scalar.activation(out=cs[:, 1, :], in_=red[:], func=ACT.Sin, scale=sgn[:])
-        nc.scalar.activation(out=cs[:, 0, :], in_=ared[:], func=ACT.Sin, scale=-1.0, bias=math.pi / 2.0)
+
+        def tables_scalar():
+            ared = tmp.tile([P, TOK], F32, name="ared", tag="ang")
+            nc.scalar.activation(out=ared[:], in_=red[:], func=ACT.Abs)
+            nc.scalar.activation(out=cs[:, 1, :], in_=red[:], func=ACT.Sin, scale=sgn[:])
+            nc.scalar.activation(out=cs[:, 0, :], in_=ared[:], func=ACT.Sin, scale=-1.0, bias=math.pi / 2.0)
 
         wide = {}
 
@@ -194,21 +201,21 @@ def tile_autoreggqaattention_pa_kernel(
             if on_vector:
                 nc.vector.tensor_scalar(
                     out=wide[c][:, k, :],
-                    in0=wb[c][:, k, :].bitcast(FP8),
+                    in0=wb[c // 2][:, k, (c % 2) * CH : (c % 2 + 1) * CH].bitcast(FP8),
                     scalar1=scale_k,
                     scalar2=None,
                     op0=ALU.mult,
                 )
             else:
                 nc.scalar.activation(
-                    out=wide[c][:, k, :], in_=wb[c][:, k, :].bitcast(FP8), func=ACT.Copy, scale=scale_k
+                    out=wide[c][:, k, :], in_=wb[c // 2][:, k, (c % 2) * CH : (c % 2 + 1) * CH].bitcast(FP8), func=ACT.Copy, scale=scale_k
                 )
 
         pending = [(c, k) for c in (1, 2, 3) for k in range(PLANES)]
 
-        def planes(count):
+        def planes(count, on_vector=False):
             for c, k in pending[0:count]:
-                widen(c, k, False)
+                widen(c, k, on_vector)
                 pending.remove((c, k))
 
         xc = keep.tile([P, PASSES, TOK], U32, name="xc", align_bytes=64)
@@ -255,7 +262,7 @@ def tile_autoreggqaattention_pa_kernel(
         ok = out_1[0].rearrange("h (p a) f -> h p (a f)", a=4)
         ov = out_2[0].rearrange("(w hh) (p b a) f -> w b p hh (a f)", hh=2, b=2, a=2)
         heads = []
-        for kind, c in (("q", 0), ("k", 0), ("q", 1), ("v", 0), ("q", 2), ("q", 3)):
+        for kind, c in ORDER:
             for hh in range(4):
                 heads.append((kind, c, hh))
         n_heads = len(heads)
@@ -434,19 +441,34 @@ def tile_autoreggqaattention_pa_kernel(
                 return units[u]
             return []
 
+        for k in C0_ON_SCALAR:
+            widen(0, k, False)
         for k in range(PLANES):
-            widen(0, k, k < C0_ON_VECTOR)
+            if k not in C0_ON_SCALAR:
+                widen(0, k, True)
         x_transposes(0)
         x_transposes(1)
+        if TABLES_AT == 0:
+            tables_scalar()
         il_scalar(0)
         il_vector(0)
+        if IL1_EARLY:
+            il_scalar(1)
+            il_vector(1)
         for g in range(PASSES):
             x_empty(0, g)
+        if TABLES_AT == 1:
+            tables_scalar()
         quant(0)
         for g in range(PASSES):
             x_empty(1, g)
-        il_scalar(1)
-        il_vector(1)
+        if TABLES_AT == 2:
+            tables_scalar()
+        if not IL1_EARLY:
+            il_scalar(1)
+            il_vector(1)
+        if TABLES_AT == 3:
+            tables_scalar()
         planes(PLANES_HEAD)
         for g in range(PASSES):
             x_quant(g)
@@ -474,6 +496,8 @@ def tile_autoreggqaattention_pa_kernel(
                     mx(j)
                 for j in back:
                     tback(j)
+            if 0 <= i + 1 < len(PLANES_STEP_V):
+                planes(PLANES_STEP_V[i + 1], True)
             if members(i + 2) and i >= 0:
                 il_vector(i + 2)
             for j in members(i):

@@ -29,10 +29,11 @@ TWO_PI_HI = 6.28125
 TWO_PI_LO = 2.0 * math.pi - TWO_PI_HI
 
 UNIT_SIZES = (2, 2, 2, 2, 2, 2, 2, 2, 2, 2, 2, 1, 1)
-S_COLS = (0, 0, 0, 16, 48, 48, 48, 48, 92, 92, 160, 32, 32)
+S_COLS = (0, 0, 0, 16, 40, 40, 40, 40, 84, 84, 152, 32, 32)
 G_COLS = (0, 0, 0, 96, 96, 96, 96, 96, 96, 48, 48, 96, 96)
 C0_ON_SCALAR = (0, 1, 2, 3, 4, 5, 12, 13, 14, 15)
 TABLES_AT = 3
+ANGLES_AT = 1
 IL1_EARLY = False
 PLANES_HEAD = 6
 PLANES_STEP = (6, 6, 5, 5, 5, 5, 5, 5, 5, 5)
@@ -149,7 +150,7 @@ def tile_autoreggqaattention_pa_kernel(
         nc.vector.tensor_copy(out=bit[:], in_=bit_i[:])
         nbit = tmp.tile([P, 7], F32, name="nbit")
         nc.vector.tensor_scalar(
-            out=nbit[:], in0=bit[:], scalar1=-1.0, scalar2=1.0, op0=ALU.mult, op1=ALU.add
+            out=nbit[:], in0=bit_i[:], scalar1=-1.0, scalar2=1.0, op0=ALU.mult, op1=ALU.add
         )
         fac = tmp.tile([P, 6], F32, name="fac")
         for b in range(6):
@@ -173,16 +174,20 @@ def tile_autoreggqaattention_pa_kernel(
         )
         sgn = tmp.tile([P, 1], F32, name="sgn")
         nc.vector.tensor_scalar(
-            out=sgn[:], in0=bit[:, 6:7], scalar1=-2.0, scalar2=1.0, op0=ALU.mult, op1=ALU.add
+            out=sgn[:], in0=bit_i[:, 6:7], scalar1=-2.0, scalar2=1.0, op0=ALU.mult, op1=ALU.add
         )
         n_i = tmp.tile([P, TOK], I32, name="n_i")
-        nc.vector.tensor_scalar(out=n_i[:], in0=tok[:], scalar1=turns[:], scalar2=None, op0=ALU.mult)
         ang = tmp.tile([P, TOK], F32, name="ang")
-        nc.vector.tensor_scalar(out=ang[:], in0=tok[:], scalar1=freq[:], scalar2=None, op0=ALU.mult)
         red = tmp.tile([P, TOK], F32, name="red")
-        nc.vector.scalar_tensor_tensor(
-            out=red[:], in0=n_i[:], scalar=-2.0 * math.pi, in1=ang[:], op0=ALU.mult, op1=ALU.add
-        )
+
+        def angles():
+            nc.vector.tensor_scalar(out=n_i[:], in0=tok[:], scalar1=turns[:], scalar2=None, op0=ALU.mult)
+            nc.vector.tensor_scalar(out=ang[:], in0=tok[:], scalar1=freq[:], scalar2=None, op0=ALU.mult)
+
+        def reduce_angles():
+            nc.vector.scalar_tensor_tensor(
+                out=red[:], in0=n_i[:], scalar=-2.0 * math.pi, in1=ang[:], op0=ALU.mult, op1=ALU.add
+            )
         cs = const.tile([P, 2, TOK], F32, name="cs")
 
         def tables_scalar():
@@ -443,9 +448,17 @@ def tile_autoreggqaattention_pa_kernel(
 
         for k in C0_ON_SCALAR:
             widen(0, k, False)
-        for k in range(PLANES):
-            if k not in C0_ON_SCALAR:
-                widen(0, k, True)
+        if ANGLES_AT == 0:
+            angles()
+            reduce_angles()
+        on_vector = [k for k in range(PLANES) if k not in C0_ON_SCALAR]
+        for k in on_vector[0 : len(on_vector) - 1]:
+            widen(0, k, True)
+        if ANGLES_AT == 1:
+            angles()
+        widen(0, on_vector[-1], True)
+        if ANGLES_AT == 1:
+            reduce_angles()
         x_transposes(0)
         x_transposes(1)
         if TABLES_AT == 0:

@@ -40,7 +40,7 @@ PLANES_STEP = (6, 6, 5, 5, 5, 5, 5, 5, 5, 5)
 X_ON_VECTOR = ()
 IL_BUFS = 2
 EVAC_LAG = 2
-TAIL_FROM = 8
+TAIL_FROM = -5
 MX_FIRST_FROM = 20
 FINE_HEADS = 1
 LOAD_ORDER = (0, "b", "x", 1, "k", 2, "v", 3)

@@ -29,12 +29,12 @@ TWO_PI_HI = 6.28125
 TWO_PI_LO = 2.0 * math.pi - TWO_PI_HI
 
 UNIT_SIZES = (2, 2, 2, 2, 2, 2, 2, 2, 2, 2, 2, 1, 1)
-S_COLS = (0, 0, 0, 16, 40, 40, 40, 40, 84, 84, 152, 32, 32)
+S_COLS = (0, 0, 0, 16, 40, 40, 40, 40, 84, 100, 176, 32, 32)
 G_COLS = (0, 0, 0, 96, 96, 96, 96, 96, 96, 48, 48, 96, 96)
-C0_ON_SCALAR = (0, 1, 2, 3, 4, 5, 12, 13, 14, 15)
+C0_ON_SCALAR = (0, 1, 2, 3, 12, 13, 14, 15)
 TABLES_AT = 3
 ANGLES_AT = 1
-IL1_EARLY = False
+IL1_EARLY = True
 PLANES_HEAD = 6
 PLANES_STEP = (6, 6, 5, 5, 5, 5, 5, 5, 5, 5)
 X_ON_VECTOR = ()
@@ -42,7 +42,7 @@ IL_BUFS = 2
 EVAC_LAG = 2
 TAIL_FROM = -5
 MX_FIRST_FROM = 20
-FINE_HEADS = 1
+FINE_HEADS = 2
 LOAD_ORDER = (0, "b", "x", 1, "k", 2, "v", 3)
 ORDER = (("q", 0), ("k", 0), ("q", 1), ("v", 0), ("q", 2), ("q", 3))
 PLANES_STEP_V = (0, 0, 0, 0, 0, 0, 0, 0, 0, 0)

@@ -29,7 +29,8 @@ TWO_PI_HI = 6.28125
 TWO_PI_LO = 2.0 * math.pi - TWO_PI_HI
 
 UNIT_SIZES = (2, 2, 2, 2, 2, 2, 2, 2, 2, 2, 2, 1, 1)
-S_COLS = (0, 0, 0, 16, 40, 40, 40, 40, 84, 100, 176, 32, 32)
+S_COLS = (0, 0, 0, 16, 40, 40, 40, 40, 88, 104, 176, 32, 32)
+RUN = 8
 G_COLS = (0, 0, 0, 96, 96, 96, 96, 96, 96, 48, 48, 96, 96)
 C0_ON_SCALAR = (0, 1, 2, 3, 12, 13, 14, 15)
 TABLES_AT = 3
@@ -308,7 +309,7 @@ def tile_autoreggqaattention_pa_kernel(
             return weights(j)[:, :, base_col + lo : base_col + hi]
 
         def il_view(u, lo, hi):
-            return columns(u, lo, hi).rearrange("p (g t) (c i) -> p g c t i", t=PACK, i=4)
+            return columns(u, lo, hi).rearrange("p (g t) (c i) -> p g c t i", t=PACK, i=RUN)
 
         def il_gpsimd(u):
             lo = n_vector(u)
@@ -327,7 +328,7 @@ def tile_autoreggqaattention_pa_kernel(
             lo = width(u) - S_COLS[u]
             if S_COLS[u] > 0:
                 nc.scalar.copy(
-                    out=il_tile(u)[:, :, lo : width(u), :].rearrange("p g (c i) t -> p g c t i", i=4),
+                    out=il_tile(u)[:, :, lo : width(u), :].rearrange("p g (c i) t -> p g c t i", i=RUN),
                     in_=il_view(u, lo, width(u)),
                 )
 
@@ -335,7 +336,7 @@ def tile_autoreggqaattention_pa_kernel(
             nv = n_vector(u)
             if nv > 0:
                 nc.vector.tensor_copy(
-                    out=il_tile(u)[:, :, 0:nv, :].rearrange("p g (c i) t -> p g c t i", i=4), in_=il_view(u, 0, nv)
+                    out=il_tile(u)[:, :, 0:nv, :].rearrange("p g (c i) t -> p g c t i", i=RUN), in_=il_view(u, 0, nv)
                 )
 
         def quant(u):

@@ -44,7 +44,7 @@ EVAC_LAG = 2
 TAIL_FROM = -5
 MX_FIRST_FROM = 20
 FINE_HEADS = 2
-LOAD_ORDER = (0, "b", "x", 1, "k", 2, "v", 3)
+LOAD_ORDER = (("q", 0, 0, 4), "b", "x", ("q", 1, 0, 2), ("k", 0, 512), ("q", 1, 2, 4), ("q", 2, 0, 4), ("v", 0, 512), ("q", 3, 0, 4))
 ORDER = (("q", 0), ("k", 0), ("q", 1), ("v", 0), ("q", 2), ("q", 3))
 PLANES_STEP_V = (0, 0, 0, 0, 0, 0, 0, 0, 0, 0)
 
@@ -89,17 +89,17 @@ def tile_autoreggqaattention_pa_kernel(
             x_a = big.tile([P, HID], BF16, name="x_a", tag="big", align_bytes=64)
             x_sb.append(x_a)
 
-        def load_q(c):
-            lo, hi = (c * CH, (c + 1) * CH) if c < 4 else ((c - 4) * 2 * CH, (c - 3) * 2 * CH)
-            for g in range(PASSES):
+        def load_q(c, g_lo, g_hi):
+            lo, hi = c * CH, (c + 1) * CH
+            for g in range(g_lo, g_hi):
                 nc.sync.dma_start(
                     out=wb[lo // (2 * CH)][:, PACK * g : PACK * (g + 1), lo % (2 * CH) : lo % (2 * CH) + hi - lo],
                     in_=wq_view[g][:, :, lo:hi],
                 )
 
-        def load_kv(dst, view):
+        def load_kv(dst, view, lo, hi):
             for g in range(PASSES):
-                nc.sync.dma_start(out=dst[:, PACK * g : PACK * (g + 1), :], in_=view[g])
+                nc.sync.dma_start(out=dst[:, PACK * g : PACK * (g + 1), lo:hi], in_=view[g][:, :, lo:hi])
 
         brow = const.tile([P, P], BF16, name="brow")
         nc.vector.memset(brow[:], 0.0)
@@ -112,12 +112,12 @@ def tile_autoreggqaattention_pa_kernel(
             elif what == "b":
                 nc.sync.dma_start(out=brow[0:16, :], in_=bq.rearrange("(h f) -> h f", f=DH))
                 nc.sync.dma_start(out=brow[16:20, :], in_=bk.rearrange("(h f) -> h f", f=DH))
-            elif what == "k":
-                load_kv(raw_k, wk_view)
-            elif what == "v":
-                load_kv(raw_v, wv_view)
+            elif what[0] == "k":
+                load_kv(raw_k, wk_view, what[1], what[2])
+            elif what[0] == "v":
+                load_kv(raw_v, wv_view, what[1], what[2])
             else:
-                load_q(what)
+                load_q(what[1], what[2], what[3])
         bv_all = const.tile([P, 4 * DH], BF16, name="bv_all")
         nc.sync.dma_start(out=bv_all[:], in_=bv.partition_broadcast(P))
 

@@ -29,9 +29,9 @@ TWO_PI_HI = 6.28125
 TWO_PI_LO = 2.0 * math.pi - TWO_PI_HI
 
 UNIT_SIZES = (2, 2, 2, 2, 2, 2, 2, 2, 2, 2, 2, 1, 1)
-S_COLS = (0, 0, 0, 16, 40, 40, 40, 40, 88, 104, 176, 32, 32)
+S_COLS = (0, 0, 0, 8, 32, 32, 32, 32, 80, 104, 176, 32, 32)
 RUN = 8
-G_COLS = (0, 0, 0, 96, 96, 96, 96, 96, 96, 48, 48, 96, 96)
+G_COLS = (0, 0, 0, 112, 112, 112, 112, 112, 112, 48, 48, 96, 96)
 C0_ON_SCALAR = (0, 1, 2, 3, 12, 13, 14, 15)
 TABLES_AT = 3
 ANGLES_AT = 1

@@ -32,8 +32,8 @@ UNIT_SIZES = (2, 2, 2, 2, 2, 2, 2, 2, 2, 2, 2, 1, 1)
 S_COLS = (0, 0, 0, 8, 32, 32, 32, 32, 80, 104, 176, 32, 32)
 RUN = 8
 G_COLS = (0, 0, 0, 112, 112, 112, 112, 112, 112, 48, 48, 96, 96)
-C0_ON_SCALAR = (0, 1, 2, 3, 12, 13, 14, 15)
-TABLES_AT = 3
+C0_ON_SCALAR = (0, 1, 4, 5, 8, 9, 12, 13)
+TABLES_AT = 0
 ANGLES_AT = 1
 IL1_EARLY = True
 PLANES_HEAD = 6

@@ -31,10 +31,11 @@ TWO_PI_LO = 2.0 * math.pi - TWO_PI_HI
 UNIT_SIZES = (2, 2, 2, 2, 2, 2, 2, 2, 2, 2, 2, 1, 1)
 S_COLS = (0, 0, 0, 8, 32, 32, 32, 32, 80, 104, 176, 32, 32)
 RUN = 8
+FIRST_SPLIT = True
 G_COLS = (0, 0, 0, 112, 112, 112, 112, 112, 112, 48, 48, 96, 96)
 C0_ON_SCALAR = (0, 1, 4, 5, 8, 9, 12, 13)
 TABLES_AT = 0
-ANGLES_AT = 1
+ANGLES_AT = 0
 IL1_EARLY = True
 PLANES_HEAD = 6
 PLANES_STEP = (6, 6, 5, 5, 5, 5, 5, 5, 5, 5)
@@ -92,10 +93,14 @@ def tile_autoreggqaattention_pa_kernel(
         def load_q(c, g_lo, g_hi):
             lo, hi = c * CH, (c + 1) * CH
             for g in range(g_lo, g_hi):
-                nc.sync.dma_start(
-                    out=wb[lo // (2 * CH)][:, PACK * g : PACK * (g + 1), lo % (2 * CH) : lo % (2 * CH) + hi - lo],
-                    in_=wq_view[g][:, :, lo:hi],
-                )
+                step = 2 if FIRST_SPLIT and c == 0 and g == 0 else PACK
+                for t in range(0, PACK, step):
+                    nc.sync.dma_start(
+                        out=wb[lo // (2 * CH)][
+                            :, PACK * g + t : PACK * g + t + step, lo % (2 * CH) : lo % (2 * CH) + hi - lo
+                        ],
+                        in_=wq_view[g][:, t : t + step, lo:hi],
+                    )
 
         def load_kv(dst, view, lo, hi):
             for g in range(PASSES):
@@ -147,43 +152,43 @@ def tile_autoreggqaattention_pa_kernel(
         nc.vector.tensor_tensor(out=bsh[:], in0=pidx[:], in1=shft[:], op=ALU.logical_shift_right)
         bit_i = tmp.tile([P, 7], I32, name="bit_i")
         nc.vector.tensor_scalar(out=bit_i[:], in0=bsh[:], scalar1=1, scalar2=None, op0=ALU.bitwise_and)
-        bit = tmp.tile([P, 7], F32, name="bit")
-        nc.vector.tensor_copy(out=bit[:], in_=bit_i[:])
-        nbit = tmp.tile([P, 7], F32, name="nbit")
-        nc.vector.tensor_scalar(
-            out=nbit[:], in0=bit_i[:], scalar1=-1.0, scalar2=1.0, op0=ALU.mult, op1=ALU.add
-        )
-        fac = tmp.tile([P, 6], F32, name="fac")
-        for b in range(6):
-            nc.vector.scalar_tensor_tensor(
+        fac = tmp.tile([P, 7], F32, name="fac")
+        for b in (5, 0, 1, 2, 3, 4):
+            nc.vector.tensor_scalar(
                 out=fac[:, b : b + 1],
-                in0=bit[:, b : b + 1],
-                scalar=ROPE_THETA ** (-(2.0**b) / 64.0),
-                in1=nbit[:, b : b + 1],
-                op0=ALU.mult,
-                op1=ALU.add,
+                in0=bit_i[:, b : b + 1],
+                scalar1=0.0,
+                scalar2=ROPE_THETA ** (-(2.0**b) / 64.0),
+                op0=ALU.is_equal,
+                op1=ALU.max,
             )
-        f3 = tmp.tile([P, 3], F32, name="f3")
-        nc.vector.tensor_tensor(out=f3[:], in0=fac[:, 0:3], in1=fac[:, 3:6], op=ALU.mult)
-        f1 = tmp.tile([P, 1], F32, name="f1")
-        nc.vector.tensor_tensor(out=f1[:], in0=f3[:, 0:1], in1=f3[:, 1:2], op=ALU.mult)
-        freq = tmp.tile([P, 1], F32, name="freq")
-        nc.vector.tensor_tensor(out=freq[:], in0=f1[:], in1=f3[:, 2:3], op=ALU.mult)
-        turns = tmp.tile([P, 1], F32, name="turns")
         nc.vector.tensor_scalar(
-            out=turns[:], in0=freq[:], scalar1=1.0 / (2.0 * math.pi), scalar2=None, op0=ALU.mult
+            out=fac[:, 6:7], in0=fac[:, 5:6], scalar1=1.0 / (2.0 * math.pi), scalar2=None, op0=ALU.mult
         )
         sgn = tmp.tile([P, 1], F32, name="sgn")
         nc.vector.tensor_scalar(
             out=sgn[:], in0=bit_i[:, 6:7], scalar1=-2.0, scalar2=1.0, op0=ALU.mult, op1=ALU.add
         )
+        f_lo = tmp.tile([P, 1], F32, name="f_lo")
+        f_hi = tmp.tile([P, 1], F32, name="f_hi")
+        f_turns = tmp.tile([P, 1], F32, name="f_turns")
+        for dst, last in ((f_lo, 2), (f_hi, 5), (f_turns, 6)):
+            first = 0 if last == 2 else 3
+            nc.vector.scalar_tensor_tensor(
+                out=dst[:],
+                in0=fac[:, first : first + 1],
+                scalar=fac[:, first + 1 : first + 2],
+                in1=fac[:, last : last + 1],
+                op0=ALU.mult,
+                op1=ALU.mult,
+            )
         n_i = tmp.tile([P, TOK], I32, name="n_i")
         ang = tmp.tile([P, TOK], F32, name="ang")
         red = tmp.tile([P, TOK], F32, name="red")
 
         def angles():
-            nc.vector.tensor_scalar(out=n_i[:], in0=tok[:], scalar1=turns[:], scalar2=None, op0=ALU.mult)
-            nc.vector.tensor_scalar(out=ang[:], in0=tok[:], scalar1=freq[:], scalar2=None, op0=ALU.mult)
+            nc.vector.tensor_scalar(out=ang[:], in0=tok[:], scalar1=f_lo[:], scalar2=f_hi[:], op0=ALU.mult, op1=ALU.mult)
+            nc.vector.tensor_scalar(out=n_i[:], in0=tok[:], scalar1=f_lo[:], scalar2=f_turns[:], op0=ALU.mult, op1=ALU.mult)
 
         def reduce_angles():
             nc.vector.scalar_tensor_tensor(

from contextlib import ExitStack
import math

import concourse.mybir as mybir
from concourse.masks import make_identity

FLOPS = 2 * 512 * 2048 * 3072

F32 = mybir.dt.float32
BF16 = mybir.dt.bfloat16
I32 = mybir.dt.int32
U32 = mybir.dt.uint32
U8 = mybir.dt.uint8
FP8 = mybir.dt.float8_e4m3fn
FP8X4 = mybir.dt.float8_e4m3fn_x4
ALU = mybir.AluOpType
ACT = mybir.ActivationFunctionType

P = 128
PACK = 4
PASSES = 4
PLANES = PASSES * PACK
TOK = 512
HID = 2048
DH = 128
CH = 512
ROPE_THETA = 10000.0
TWO_PI_HI = 6.28125
TWO_PI_LO = 2.0 * math.pi - TWO_PI_HI

UNIT_SIZES = (2, 2, 2, 2, 2, 2, 2, 2, 2, 2, 2, 1, 1)
S_COLS = (0, 0, 0, 8, 32, 32, 32, 32, 80, 104, 176, 32, 32)
RUN = 8
FIRST_SPLIT = True
G_COLS = (0, 0, 0, 112, 112, 112, 112, 112, 112, 48, 48, 96, 96)
C0_ON_SCALAR = (0, 1, 4, 5, 8, 9, 12, 13)
TABLES_AT = 0
ANGLES_AT = 0
IL1_EARLY = True
PLANES_HEAD = 6
PLANES_STEP = (6, 6, 5, 5, 5, 5, 5, 5, 5, 5)
X_ON_VECTOR = ()
IL_BUFS = 2
EVAC_LAG = 2
TAIL_FROM = -5
MX_FIRST_FROM = 20
FINE_HEADS = 2
LOAD_ORDER = (("q", 0, 0, 4), "b", "x", ("q", 1, 0, 2), ("k", 0, 512), ("q", 1, 2, 4), ("q", 2, 0, 4), ("v", 0, 512), ("q", 3, 0, 4))
ORDER = (("q", 0), ("k", 0), ("q", 1), ("v", 0), ("q", 2), ("q", 3))
PLANES_STEP_V = (0, 0, 0, 0, 0, 0, 0, 0, 0, 0)


def tile_autoreggqaattention_pa_kernel(
    tc, hidden_states, Wq_bytes, Wq_scale, bq, Wk, bk, Wv, bv, out_0, out_1, out_2
):
    nc = tc.nc
    with ExitStack() as ctx:
        const = ctx.enter_context(tc.tile_pool(name="const", bufs=1))
        tmp = ctx.enter_context(tc.tile_pool(name="tmp", bufs=1))
        big = ctx.enter_context(tc.tile_pool(name="big", bufs=5))
        small = ctx.enter_context(tc.tile_pool(name="small", bufs=6))
        wbp = ctx.enter_context(tc.tile_pool(name="wbp", bufs=1))
        rawp = ctx.enter_context(tc.tile_pool(name="rawp", bufs=1))
        widep = ctx.enter_context(tc.tile_pool(name="widep", bufs=3))
        ilp = ctx.enter_context(tc.tile_pool(name="ilp", bufs=IL_BUFS))
        cod = ctx.enter_context(tc.tile_pool(name="cod", bufs=4))
        keep = ctx.enter_context(tc.tile_pool(name="keep", bufs=1))
        ps_acc = ctx.enter_context(tc.psum_pool(name="ps_acc", bufs=4))
        ps_tr = ctx.enter_context(tc.psum_pool(name="ps_tr", bufs=4))
        ctx.enter_context(tc.manual_schedule())

        wscale = const.tile([P, PASSES, PACK], F32, name="wscale")
        nc.sync.dma_start(
            out=wscale[:],
            in_=Wq_scale.rearrange("(g p t) o -> p g (t o)", g=PASSES, p=P, t=PACK),
        )
        wq_view = Wq_bytes.rearrange("(g p t) n -> g p t n", g=PASSES, p=P, t=PACK)
        wk_view = Wk.rearrange("(g p t) n -> g p t n", g=PASSES, p=P, t=PACK)
        wv_view = Wv.rearrange("(g p t) n -> g p t n", g=PASSES, p=P, t=PACK)
        hs = hidden_states[0].rearrange("(p a) h -> a p h", a=4)

        wb = []
        for c in range(2):
            wb_c = wbp.tile([P, PLANES, 2 * CH], U8, name="wb%d" % c, tag="wb%d" % c)
            wb.append(wb_c)
        raw_k = rawp.tile([P, PLANES, CH], BF16, name="raw_k", tag="raw_k")
        raw_v = rawp.tile([P, PLANES, CH], BF16, name="raw_v", tag="raw_v")
        x_sb = []
        for a in range(4):
            x_a = big.tile([P, HID], BF16, name="x_a", tag="big", align_bytes=64)
            x_sb.append(x_a)

        def load_q(c, g_lo, g_hi):
            lo, hi = c * CH, (c + 1) * CH
            for g in range(g_lo, g_hi):
                step = 2 if FIRST_SPLIT and c == 0 and g == 0 else PACK
                for t in range(0, PACK, step):
                    nc.sync.dma_start(
                        out=wb[lo // (2 * CH)][
                            :, PACK * g + t : PACK * g + t + step, lo % (2 * CH) : lo % (2 * CH) + hi - lo
                        ],
                        in_=wq_view[g][:, t : t + step, lo:hi],
                    )

        def load_kv(dst, view, lo, hi):
            for g in range(PASSES):
                nc.sync.dma_start(out=dst[:, PACK * g : PACK * (g + 1), lo:hi], in_=view[g][:, :, lo:hi])

        brow = const.tile([P, P], BF16, name="brow")
        nc.vector.memset(brow[:], 0.0)
        zero1 = const.tile([P, 1], F32, name="zero1")
        nc.vector.memset(zero1[:], 0.0)
        for what in LOAD_ORDER:
            if what == "x":
                for a in range(4):
                    nc.sync.dma_start(out=x_sb[a][:], in_=hs[a])
            elif what == "b":
                nc.sync.dma_start(out=brow[0:16, :], in_=bq.rearrange("(h f) -> h f", f=DH))
                nc.sync.dma_start(out=brow[16:20, :], in_=bk.rearrange("(h f) -> h f", f=DH))
            elif what[0] == "k":
                load_kv(raw_k, wk_view, what[1], what[2])
            elif what[0] == "v":
                load_kv(raw_v, wv_view, what[1], what[2])
            else:
                load_q(what[1], what[2], what[3])
        bv_all = const.tile([P, 4 * DH], BF16, name="bv_all")
        nc.sync.dma_start(out=bv_all[:], in_=bv.partition_broadcast(P))

        warm = const.tile([P, 1], F32, name="warm")
        nc.scalar.activation(out=warm[:], in_=zero1[:], func=ACT.Sin)
        pidx = tmp.tile([P, 7], I32, name="pidx")
        nc.gpsimd.iota(pidx[:], pattern=[[0, 7]], base=0, channel_multiplier=1)
        shft = tmp.tile([P, 7], I32, name="shft")
        nc.gpsimd.iota(shft[:], pattern=[[1, 7]], base=0, channel_multiplier=0)
        tok = tmp.tile([P, TOK], F32, name="tok")
        nc.gpsimd.iota(
            tok[:],
            pattern=[[1, 4], [4, P]],
            base=0,
            channel_multiplier=0,
            allow_small_or_imprecise_dtypes=True,
        )
        ident_bf = const.tile([P, P], BF16, name="ident_bf")
        make_identity(nc, ident_bf[:])
        ident = const.tile([P, P], F32, name="ident")
        make_identity(nc, ident[:])
        swap = const.tile([P, P], F32, name="swap")
        nc.gpsimd.tensor_copy(out=swap[:, 0:64], in_=ident[:, 64:128])
        nc.gpsimd.tensor_copy(out=swap[:, 64:128], in_=ident[:, 0:64])

        bsh = tmp.tile([P, 7], I32, name="bsh")
        nc.vector.tensor_tensor(out=bsh[:], in0=pidx[:], in1=shft[:], op=ALU.logical_shift_right)
        bit_i = tmp.tile([P, 7], I32, name="bit_i")
        nc.vector.tensor_scalar(out=bit_i[:], in0=bsh[:], scalar1=1, scalar2=None, op0=ALU.bitwise_and)
        fac = tmp.tile([P, 7], F32, name="fac")
        for b in (5, 0, 1, 2, 3, 4):
            nc.vector.tensor_scalar(
                out=fac[:, b : b + 1],
                in0=bit_i[:, b : b + 1],
                scalar1=0.0,
                scalar2=ROPE_THETA ** (-(2.0**b) / 64.0),
                op0=ALU.is_equal,
                op1=ALU.max,
            )
        nc.vector.tensor_scalar(
            out=fac[:, 6:7], in0=fac[:, 5:6], scalar1=1.0 / (2.0 * math.pi), scalar2=None, op0=ALU.mult
        )
        sgn = tmp.tile([P, 1], F32, name="sgn")
        nc.vector.tensor_scalar(
            out=sgn[:], in0=bit_i[:, 6:7], scalar1=-2.0, scalar2=1.0, op0=ALU.mult, op1=ALU.add
        )
        f_lo = tmp.tile([P, 1], F32, name="f_lo")
        f_hi = tmp.tile([P, 1], F32, name="f_hi")
        f_turns = tmp.tile([P, 1], F32, name="f_turns")
        for dst, last in ((f_lo, 2), (f_hi, 5), (f_turns, 6)):
            first = 0 if last == 2 else 3
            nc.vector.scalar_tensor_tensor(
                out=dst[:],
                in0=fac[:, first : first + 1],
                scalar=fac[:, first + 1 : first + 2],
                in1=fac[:, last : last + 1],
                op0=ALU.mult,
                op1=ALU.mult,
            )
        n_i = tmp.tile([P, TOK], I32, name="n_i")
        ang = tmp.tile([P, TOK], F32, name="ang")
        red = tmp.tile([P, TOK], F32, name="red")

        def angles():
            nc.vector.tensor_scalar(out=ang[:], in0=tok[:], scalar1=f_lo[:], scalar2=f_hi[:], op0=ALU.mult, op1=ALU.mult)
            nc.vector.tensor_scalar(out=n_i[:], in0=tok[:], scalar1=f_lo[:], scalar2=f_turns[:], op0=ALU.mult, op1=ALU.mult)

        def reduce_angles():
            nc.vector.scalar_tensor_tensor(
                out=red[:], in0=n_i[:], scalar=-2.0 * math.pi, in1=ang[:], op0=ALU.mult, op1=ALU.add
            )
        cs = const.tile([P, 2, TOK], F32, name="cs")

        def tables_scalar():
            ared = tmp.tile([P, TOK], F32, name="ared", tag="ang")
            nc.scalar.activation(out=ared[:], in_=red[:], func=ACT.Abs)
            nc.scalar.activation(out=cs[:, 1, :], in_=red[:], func=ACT.Sin, scale=sgn[:])
            nc.scalar.activation(out=cs[:, 0, :], in_=ared[:], func=ACT.Sin, scale=-1.0, bias=math.pi / 2.0)

        wide = {}

        def widen(c, k, on_vector):
            if c not in wide:
                wide_c = widep.tile([P, PLANES, CH], BF16, name="wide", tag="wide")
                wide[c] = wide_c
            scale_k = wscale[:, k // PACK, k % PACK : k % PACK + 1]
            if on_vector:
                nc.vector.tensor_scalar(
                    out=wide[c][:, k, :],
                    in0=wb[c // 2][:, k, (c % 2) * CH : (c % 2 + 1) * CH].bitcast(FP8),
                    scalar1=scale_k,
                    scalar2=None,
                    op0=ALU.mult,
                )
            else:
                nc.scalar.activation(
                    out=wide[c][:, k, :], in_=wb[c // 2][:, k, (c % 2) * CH : (c % 2 + 1) * CH].bitcast(FP8), func=ACT.Copy, scale=scale_k
                )

        pending = [(c, k) for c in (1, 2, 3) for k in range(PLANES)]

        def planes(count, on_vector=False):
            for c, k in pending[0:count]:
                widen(c, k, on_vector)
                pending.remove((c, k))

        xc = keep.tile([P, PASSES, TOK], U32, name="xc", align_bytes=64)
        xs = keep.tile([P, PASSES, TOK], U8, name="xs", align_bytes=64)
        banks = {}
        grouped = {}

        def x_transposes(jp):
            for g in range(PASSES):
                if jp == 0:
                    xt = ps_tr.tile([P, 2, 256], F32, name="xt", tag="tr")
                else:
                    xt = ps_acc.tile([P, 2, 256], F32, name="xt", tag="acc")
                banks[(jp, g)] = xt
            for al in range(2):
                words = x_sb[2 * jp + al][:].bitcast(F32)
                for g in range(PASSES):
                    for u in range(2):
                        nc.tensor.transpose(
                            banks[(jp, g)][:, u, al * P : (al + 1) * P],
                            words[:, 256 * g + u : 256 * (g + 1) : 2],
                            ident[:],
                        )

        def x_empty(jp, g):
            if g not in grouped:
                xg = big.tile([P, TOK, PACK], BF16, name="xg", tag="big", align_bytes=64)
                grouped[g] = xg
            half = grouped[g][:, jp * 256 : (jp + 1) * 256, :]
            xg_words = half.rearrange("p r t -> p (r t)").bitcast(F32).rearrange("p (r u) -> p r u", u=2)
            if (jp, g) in X_ON_VECTOR:
                nc.vector.tensor_copy(out=xg_words, in_=banks[(jp, g)][:].rearrange("p u r -> p r u"))
            else:
                nc.scalar.copy(out=xg_words, in_=banks[(jp, g)][:].rearrange("p u r -> p r u"))

        def x_quant(g):
            nc.vector.quantize_mx(
                out=xc[:, g, :].bitcast(FP8X4),
                scales=xs[:, g, :],
                in_=grouped[g][:].rearrange("p r t -> p (r t)"),
            )

        oq = out_0[0].rearrange("h (p a) f -> h p (a f)", a=4)
        ok = out_1[0].rearrange("h (p a) f -> h p (a f)", a=4)
        ov = out_2[0].rearrange("(w hh) (p b a) f -> w b p hh (a f)", hh=2, b=2, a=2)
        heads = []
        for kind, c in ORDER:
            for hh in range(4):
                heads.append((kind, c, hh))
        n_heads = len(heads)
        units = []
        unit_of = {}
        for size in UNIT_SIZES:
            first = sum([len(hs_u) for hs_u in units])
            units.append(list(range(first, first + size)))
            for j in units[-1]:
                unit_of[j] = len(units) - 1
        n_units = len(units)
        assert sum(UNIT_SIZES) == n_heads
        state = {}

        def weights(j):
            kind, c, hh = heads[j]
            if kind == "q":
                return wide[c]
            if kind == "k":
                return raw_k
            return raw_v

        def width(u):
            return DH * len(units[u])

        def n_vector(u):
            return width(u) - G_COLS[u] - S_COLS[u]

        def il_tile(u):
            if ("il", u) not in state:
                il = ilp.tile([P, PASSES, width(u), PACK], BF16, name="il", tag="il", align_bytes=64)
                state[("il", u)] = il
            return state[("il", u)]

        def columns(u, lo, hi):
            j = units[u][0]
            base_col = heads[j][2] * DH
            return weights(j)[:, :, base_col + lo : base_col + hi]

        def il_view(u, lo, hi):
            return columns(u, lo, hi).rearrange("p (g t) (c i) -> p g c t i", t=PACK, i=RUN)

        def il_gpsimd(u):
            lo = n_vector(u)
            hi = lo + G_COLS[u]
            if hi > lo:
                nc.gpsimd.tensor_scalar(
                    out=il_tile(u)[:, :, lo:hi, :],
                    in0=columns(u, lo, hi).rearrange("p (g t) n -> p g n t", t=PACK),
                    scalar1=1.0,
                    scalar2=0.0,
                    op0=ALU.mult,
                    op1=ALU.add,
                )

        def il_scalar(u):
            lo = width(u) - S_COLS[u]
            if S_COLS[u] > 0:
                nc.scalar.copy(
                    out=il_tile(u)[:, :, lo : width(u), :].rearrange("p g (c i) t -> p g c t i", i=RUN),
                    in_=il_view(u, lo, width(u)),
                )

        def il_vector(u):
            nv = n_vector(u)
            if nv > 0:
                nc.vector.tensor_copy(
                    out=il_tile(u)[:, :, 0:nv, :].rearrange("p g (c i) t -> p g c t i", i=RUN), in_=il_view(u, 0, nv)
                )

        def quant(u):
            wc = cod.tile([P, PASSES * width(u)], U32, name="wc", tag="wc", align_bytes=64)
            ws = cod.tile([P, PASSES * width(u)], U8, name="ws", tag="ws", align_bytes=64)
            nc.vector.quantize_mx(
                out=wc[:].bitcast(FP8X4),
                scales=ws[:],
                in_=il_tile(u)[:].rearrange("p g n t -> p (g n t)"),
            )
            state[("wc", u)] = wc
            state[("ws", u)] = ws

        def pieces(j):
            if j >= n_heads - FINE_HEADS:
                return [slice(0, TOK // 2), slice(TOK // 2, TOK)]
            return [slice(0, TOK)]

        def mx(j):
            u = unit_of[j]
            place = j - units[u][0]
            acc = ps_acc.tile([P, TOK], F32, name="acc", tag="acc")
            wc, ws = state[("wc", u)], state[("ws", u)]
            state[("acc", j)] = acc
            if heads[j][0] == "v":
                for a in range(2):
                    blk = slice((2 * place + a) * P, (2 * place + a + 1) * P)
                    for g in range(PASSES):
                        cols = slice(g * width(u), (g + 1) * width(u))
                        nc.tensor.matmul_mx(
                            out=acc[:, a * 2 * DH : (a + 1) * 2 * DH],
                            lhsT=xc[:, g, blk].bitcast(FP8X4),
                            lhsT_scale=xs[:, g, blk],
                            rhs=wc[:, cols].bitcast(FP8X4),
                            rhs_scale=ws[:, cols],
                            start=(g == 0),
                            stop=(g == PASSES - 1),
                        )
                return
            for g in range(PASSES):
                cols = slice(g * width(u) + place * DH, g * width(u) + (place + 1) * DH)
                nc.tensor.matmul_mx(
                    out=acc[:],
                    lhsT=wc[:, cols].bitcast(FP8X4),
                    lhsT_scale=ws[:, cols],
                    rhs=xc[:, g, :].bitcast(FP8X4),
                    rhs_scale=xs[:, g, :],
                    start=(g == 0),
                    stop=(g == PASSES - 1),
                )

        def rope(j):
            kind, c, hh = heads[j]
            acc = state[("acc", j)]
            if kind == "v":
                first_col = (hh // 2) * 2 * DH
                ob = small.tile([P, 2, 2, DH], F32, name="ob", tag="small", align_bytes=64)
                nc.vector.tensor_tensor(
                    out=ob[:].rearrange("p hh a f -> p a hh f"),
                    in0=acc[:].rearrange("p (a hh f) -> p a hh f", a=2, hh=2),
                    in1=bv_all[:, first_col : first_col + 2 * DH]
                    .rearrange("p (hh f) -> p hh f", hh=2)
                    .unsqueeze(1)
                    .to_broadcast([P, 2, 2, DH]),
                    op=ALU.add,
                )
                nc.sync.dma_start(out=ov[hh // 2][hh % 2], in_=ob[:].rearrange("p hh a f -> p hh (a f)"))
                return
            bcol = 4 * c + hh if kind == "q" else 16 + hh
            uw = big.tile([P, 2, TOK], F32, name="uw", tag="big", align_bytes=64)
            state[("uw", j)] = uw
            for cols in pieces(j):
                nc.vector.scalar_tensor_tensor(
                    out=uw[:, :, cols],
                    in0=acc[:, cols].unsqueeze(1).to_broadcast([P, 2, cols.stop - cols.start]),
                    scalar=bias[:, bcol : bcol + 1],
                    in1=cs[:, :, cols],
                    op0=ALU.add,
                    op1=ALU.mult,
                )

        def tback(j):
            if heads[j][0] == "v":
                return
            tr = ps_tr.tile([P, TOK], F32, name="tr", tag="tr")
            state[("tr", j)] = tr
            uw = state[("uw", j)]
            for a in range(4):
                blk = slice(a * P, (a + 1) * P)
                nc.tensor.matmul(
                    tr[:, blk], lhsT=uw[:, 0, blk], rhs=ident[:], start=True, stop=False, is_transpose=True
                )
                nc.tensor.matmul(
                    tr[:, blk], lhsT=uw[:, 1, blk], rhs=swap[:], start=False, stop=True, is_transpose=True
                )

        def evac(j):
            kind, c, hh = heads[j]
            if kind == "v":
                return
            ob = small.tile([P, TOK], F32, name="ob", tag="small", align_bytes=64)
            for cols in pieces(j):
                nc.scalar.copy(out=ob[:, cols], in_=state[("tr", j)][:, cols])
                nc.sync.dma_start(out=(oq[4 * c + hh] if kind == "q" else ok[hh])[:, cols], in_=ob[:, cols])

        def members(u):
            if 0 <= u < n_units:
                return units[u]
            return []

        for k in C0_ON_SCALAR:
            widen(0, k, False)
        if ANGLES_AT == 0:
            angles()
            reduce_angles()
        on_vector = [k for k in range(PLANES) if k not in C0_ON_SCALAR]
        for k in on_vector[0 : len(on_vector) - 1]:
            widen(0, k, True)
        if ANGLES_AT == 1:
            angles()
        widen(0, on_vector[-1], True)
        if ANGLES_AT == 1:
            reduce_angles()
        x_transposes(0)
        x_transposes(1)
        if TABLES_AT == 0:
            tables_scalar()
        il_scalar(0)
        il_vector(0)
        if IL1_EARLY:
            il_scalar(1)
            il_vector(1)
        for g in range(PASSES):
            x_empty(0, g)
        if TABLES_AT == 1:
            tables_scalar()
        quant(0)
        for g in range(PASSES):
            x_empty(1, g)
        if TABLES_AT == 2:
            tables_scalar()
        if not IL1_EARLY:
            il_scalar(1)
            il_vector(1)
        if TABLES_AT == 3:
            tables_scalar()
        planes(PLANES_HEAD)
        for g in range(PASSES):
            x_quant(g)
        bias_ps = ps_tr.tile([P, P], BF16, name="bias_ps", tag="tr")
        nc.tensor.transpose(bias_ps[:], brow[:], ident_bf[:])
        bias = const.tile([P, 20], F32, name="bias")
        nc.vector.tensor_copy(out=bias[:], in_=bias_ps[:, 0:20])
        quant(1)
        il_scalar(2)
        for i in range(-1, n_units + 1 + EVAC_LAG):
            back, ahead = members(i - 1), members(i + 1)
            if i < TAIL_FROM:
                for k in range(2):
                    for j in back[k : k + 1]:
                        tback(j)
                    for j in ahead[k : k + 1]:
                        mx(j)
            elif i < MX_FIRST_FROM:
                for j in back:
                    tback(j)
                for j in ahead:
                    mx(j)
            else:
                for j in ahead:
                    mx(j)
                for j in back:
                    tback(j)
            if 0 <= i + 1 < len(PLANES_STEP_V):
                planes(PLANES_STEP_V[i + 1], True)
            if members(i + 2) and i >= 0:
                il_vector(i + 2)
            for j in members(i):
                rope(j)
            if members(i + 2) and i >= 0:
                quant(i + 2)
            if 0 <= i + 1 < len(PLANES_STEP):
                planes(PLANES_STEP[i + 1])
            if members(i + 3):
                il_gpsimd(i + 3)
                il_scalar(i + 3)
            for j in members(i - EVAC_LAG):
                evac(j)
